import numpy as np
import ml_dtypes


def mxq(x, axis, fmt="e4m3"):
    dtype, down = {"e4m3": (ml_dtypes.float8_e4m3fn, 7), "e5m2": (ml_dtypes.float8_e5m2, 14)}[fmt]
    v = np.moveaxis(np.asarray(x, np.float32).astype(ml_dtypes.bfloat16).astype(np.float64), axis, -1)
    blocks = v.reshape(v.shape[:-1] + (-1, 32))
    amax = np.abs(blocks).max(-1, keepdims=True)
    byte = np.maximum(np.where(amax > 0, np.frexp(amax)[1] - 1 + 127, 0) - down, 1)
    scale = np.exp2(byte - 127.0)
    codes = (blocks / scale).astype(np.float32).astype(dtype).astype(np.float64)
    return np.moveaxis((codes * scale).reshape(v.shape), -1, axis)


WIDE = False


def mx_kscale(k):
    if not WIDE:
        return np.ones(k)
    levels = np.array([30, -30])
    if k % 512:
        return np.exp2(np.random.permutation(np.resize(levels, k // 32))).repeat(32)
    a = np.empty((k // 512, 16))
    for p in range(k // 512):
        a[p, :8] = np.random.permutation(np.resize(levels, 8))
        for g in range(8):
            far = levels[np.abs(levels - a[p, g]) >= 10]
            a[p, g + 8] = far[np.random.randint(len(far))]
    return np.exp2(a.ravel()).repeat(32)


BF16 = ml_dtypes.bfloat16


def bf(x):
    return np.asarray(x, np.float32).astype(BF16)


def f64(x):
    return np.asarray(x).astype(np.float64)


B, S, DIM, H, NKV, HD, GS = 1, 512, 2048, 16, 4, 128, 128
QS = H * HD
KVS = NKV * HD
HALF = HD // 2
ROPE_BASE = 10000.0
RMS_EPS = 1.1920929e-07


def rms_norm(v):
    return v / np.sqrt(np.mean(v * v, axis=-1, keepdims=True) + RMS_EPS)


def rope_cos_sin():
    inv_freq = 1.0 / ROPE_BASE ** (np.arange(0, HD, 2) / HD)
    freqs = np.outer(np.arange(S), inv_freq)
    return np.cos(freqs)[None, :, None, :], np.sin(freqs)[None, :, None, :]


def apply_rotary_emb(u, cos, sin):
    u1, u2 = u[..., :HALF], u[..., HALF:]
    return np.concatenate((u1 * cos + u2 * sin, u1 * -sin + u2 * cos), axis=-1)


def setup_inputs():
    s = mx_kscale(DIM)
    return {"x": bf(np.random.standard_normal((B, S, DIM)) * s),
            "w_qkv_tern": bf(np.random.standard_normal((QS + 2 * KVS, DIM)) * 0.66 / np.sqrt(DIM) / s[None, :]),
            "q_gain": bf(1.0 + 0.1 * np.random.standard_normal(H))}


def reference(x, w_qkv_tern, q_gain):
    qkv = mxq(f64(x), 2, "e5m2") @ mxq(f64(w_qkv_tern), 1, "e5m2").T
    q = qkv[..., :QS].reshape(B, S, H, HD)
    k = qkv[..., QS:QS + KVS].reshape(B, S, NKV, HD)
    v = qkv[..., QS + KVS:].reshape(B, S, NKV, HD)
    q, k = rms_norm(q), rms_norm(k)
    cos, sin = rope_cos_sin()
    q = apply_rotary_emb(q, cos, sin)
    k = apply_rotary_emb(k, cos, sin)
    q = q * f64(q_gain)[None, None, :, None]
    return q, k, v

@@ -1,0 +1,274 @@
+from contextlib import ExitStack
+
+import concourse.mybir as mybir
+from concourse.masks import make_identity
+
+F32 = mybir.dt.float32
+BF16 = mybir.dt.bfloat16
+I32 = mybir.dt.int32
+U32 = mybir.dt.uint32
+U8 = mybir.dt.uint8
+E5X4 = mybir.dt.float8_e5m2_x4
+ACT = mybir.ActivationFunctionType
+ALU = mybir.AluOpType
+
+P = 128
+K = 2048
+PASSES = 4
+TOKENS = 512
+HEAD = 128
+HALF = 64
+CHUNK = 512
+N_UNITS = 14
+X_UNITS = 2
+HEAD_UNITS = 5
+N_GROUPS = 12
+ROPE_GROUPS = 10
+RMS_EPS = 1.1920929e-07
+PI = 3.141592653589793
+PI_HI = 102944.0 / 32768.0
+PI_LO = PI - PI_HI
+FREQ_RATIO = 10000.0 ** (-1.0 / 64.0)
+
+FLOPS = 2 * TOKENS * K * 3072
+
+
+def tile_causalselfattention_pa_kernel(tc, x, w_qkv_tern, q_gain, out_0, out_1, out_2):
+    nc = tc.nc
+    x_rows = x.rearrange("b s k -> (b s) k")
+    row_tiles = [x_rows[P * i : P * (i + 1), :] for i in range(4)]
+    row_tiles.extend([w_qkv_tern[P * i : P * (i + 1), :] for i in range(24)])
+    q_flat = out_0.rearrange("b s h d -> (b s) (h d)")
+    dests = [q_flat[:, CHUNK * c : CHUNK * (c + 1)] for c in range(4)]
+    dests.append(out_1.rearrange("b s h d -> (b s) (h d)"))
+    dests.append(out_2.rearrange("b s h d -> (b s) (h d)"))
+
+    with ExitStack() as ctx:
+        const = ctx.enter_context(tc.tile_pool(name="const", bufs=1))
+        rawp = ctx.enter_context(tc.tile_pool(name="rawp", bufs=28))
+        grpp = ctx.enter_context(tc.tile_pool(name="grpp", bufs=8))
+        codep = ctx.enter_context(tc.tile_pool(name="codep", bufs=3))
+        epi = ctx.enter_context(tc.tile_pool(name="epi", bufs=2))
+        outp = ctx.enter_context(tc.tile_pool(name="outp", bufs=6))
+        tps = ctx.enter_context(tc.psum_pool(name="tps", bufs=4))
+        accs = ctx.enter_context(tc.psum_pool(name="accs", bufs=4))
+        ctx.enter_context(tc.manual_schedule())
+
+        gain_bf = const.tile([P, 16], BF16, name="gain_bf")
+        raws = []
+        for i in range(28):
+            raw = rawp.tile([P, K], BF16, name="raw", tag="raw")
+            nc.sync.dma_start(out=raw[:], in_=row_tiles[i])
+            raws.append(raw)
+            if i == 2 * HEAD_UNITS - 1:
+                nc.sync.dma_start(out=gain_bf[:], in_=q_gain.partition_broadcast(P))
+
+        t_int = const.tile([P, 4], I32, name="t_int")
+        nc.gpsimd.iota(t_int[:], pattern=[[P, 4]], base=0, channel_multiplier=1)
+        ident = const.tile([P, P], F32, name="ident")
+        make_identity(nc, ident[:])
+        neg_half = const.tile([P, 8], F32, name="neg_half")
+        nc.gpsimd.memset(neg_half[:], -0.5)
+        gain = const.tile([P, 20], F32, name="gain")
+        nc.gpsimd.memset(gain[:], 1.0)
+
+        half_ang = const.tile([P, 4, HALF], F32, name="half_ang")
+        nc.vector.tensor_scalar(
+            out=half_ang[:, :, 0:1], in0=t_int[:].unsqueeze(2), scalar1=0.5, scalar2=None, op0=ALU.mult
+        )
+        for width in (1, 4, 16):
+            for m in range(1, 4):
+                nc.vector.tensor_scalar(
+                    out=half_ang[:, :, m * width : (m + 1) * width],
+                    in0=half_ang[:, :, 0:width],
+                    scalar1=FREQ_RATIO ** (m * width),
+                    scalar2=None,
+                    op0=ALU.mult,
+                )
+        turns = const.tile([P, 4, HALF], I32, name="turns")
+        nc.vector.tensor_scalar(
+            out=turns[:], in0=half_ang[:], scalar1=1.0 / PI, scalar2=0.1, op0=ALU.mult, op1=ALU.add
+        )
+        red_hi = const.tile([P, 4, HALF], F32, name="red_hi")
+        nc.vector.scalar_tensor_tensor(
+            out=red_hi[:], in0=turns[:], scalar=-PI_HI, in1=half_ang[:], op0=ALU.mult, op1=ALU.add
+        )
+        red = const.tile([P, 4, HALF], F32, name="red")
+        nc.vector.scalar_tensor_tensor(
+            out=red[:], in0=turns[:], scalar=-PI_LO, in1=red_hi[:], op0=ALU.mult, op1=ALU.add
+        )
+        sin_a = const.tile([P, 4, HALF], F32, name="sin_a")
+        nc.scalar.activation(out=sin_a[:], in_=red[:], func=ACT.Sin)
+        sin_b = const.tile([P, 4, HALF], F32, name="sin_b")
+        nc.scalar.activation(out=sin_b[:], in_=red[:], func=ACT.Sin, bias=-PI / 4.0)
+        sq_a = const.tile([P, 4, HALF], F32, name="sq_a")
+        nc.gpsimd.tensor_tensor(out=sq_a[:], in0=sin_a[:], in1=sin_a[:], op=ALU.mult)
+        sq_b = const.tile([P, 4, HALF], F32, name="sq_b")
+        nc.gpsimd.tensor_tensor(out=sq_b[:], in0=sin_b[:], in1=sin_b[:], op=ALU.mult)
+        tab = const.tile([P, 4, 2, HEAD], F32, name="tab")
+        for row, lo, src, sign in ((0, 0, sq_a, 1.0), (0, HALF, sq_a, 1.0), (1, 0, sq_b, -1.0), (1, HALF, sq_b, 1.0)):
+            nc.gpsimd.tensor_scalar(
+                out=tab[:, :, row, lo : lo + HALF],
+                in0=src[:],
+                scalar1=-2.0 * sign,
+                scalar2=sign,
+                op0=ALU.mult,
+                op1=ALU.add,
+            )
+        nc.gpsimd.tensor_copy(out=gain[:, 0:16], in_=gain_bf[:])
+
+        junk = const.tile([P, HEAD], BF16, name="junk")
+        x_codes = const.tile([P, PASSES, TOKENS], U32, name="x_codes", align_bytes=64)
+        x_scales = const.tile([P, PASSES, TOKENS], U8, name="x_scales", align_bytes=64)
+
+        state = {}
+
+        def transposes(s):
+            banks = [tps.tile([P, 2, 2 * P], F32, name="tp", tag="tp") for g in range(PASSES)]
+            for r in range(2):
+                words = raws[2 * s + r][:].bitcast(F32)
+                for g in range(PASSES):
+                    for u in range(2):
+                        nc.tensor.transpose(
+                            banks[g][:, u, P * r : P * (r + 1)],
+                            words[:, 256 * g + u : 256 * (g + 1) : 2],
+                            ident[:],
+                        )
+            state["banks"] = banks
+
+        def copies(s):
+            groups = []
+            for g in range(PASSES):
+                grp = grpp.tile([P, 8 * P], BF16, name="grp", tag="grp", align_bytes=64)
+                dst = grp[:].bitcast(F32).rearrange("p (n u) -> p n u", u=2)
+                src = state["banks"][g][:].rearrange("p u n -> p n u")
+                if s < HEAD_UNITS and g == PASSES - 1:
+                    nc.vector.tensor_copy(out=dst, in_=src)
+                else:
+                    nc.scalar.copy(out=dst, in_=src)
+                groups.append(grp)
+            state["groups"] = groups
+
+        def quantise(s):
+            if s < X_UNITS:
+                codes, scales, lo = x_codes, x_scales, 2 * P * s
+            else:
+                if (s - X_UNITS) % 2 == 0:
+                    state["w_codes", (s - X_UNITS) // 2] = codep.tile(
+                        [P, PASSES, CHUNK], U32, name="w_codes", tag="w_codes", align_bytes=64
+                    )
+                    state["w_scales", (s - X_UNITS) // 2] = codep.tile(
+                        [P, PASSES, CHUNK], U8, name="w_scales", tag="w_scales", align_bytes=64
+                    )
+                codes = state["w_codes", (s - X_UNITS) // 2]
+                scales = state["w_scales", (s - X_UNITS) // 2]
+                lo = 2 * P * ((s - X_UNITS) % 2)
+            for g in range(PASSES):
+                nc.vector.quantize_mx(
+                    out=codes[:, g, lo : lo + 2 * P].bitcast(E5X4),
+                    scales=scales[:, g, lo : lo + 2 * P],
+                    in_=state["groups"][g][:],
+                )
+
+        def matmuls(j):
+            c = j // 2
+            sums = []
+            for mi in range(2):
+                m = 2 * (j % 2) + mi
+                if j < ROPE_GROUPS:
+                    acc = accs.tile([P, CHUNK], F32, name="acc", tag="acc")
+                else:
+                    acc = tps.tile([P, CHUNK], F32, name="tp", tag="tp")
+                for g in range(PASSES):
+                    nc.tensor.matmul_mx(
+                        out=acc[:],
+                        lhsT=x_codes[:, g, P * m : P * (m + 1)].bitcast(E5X4),
+                        lhsT_scale=x_scales[:, g, P * m : P * (m + 1)],
+                        rhs=state["w_codes", c][:, g, :].bitcast(E5X4),
+                        rhs_scale=state["w_scales", c][:, g, :],
+                        start=(g == 0),
+                        stop=(g == PASSES - 1),
+                    )
+                sums.append(acc)
+            state["sums", j] = sums
+
+        def squares(j):
+            ssq = epi.tile([P, 8], F32, name="ssq", tag="ssq")
+            for mi in range(2):
+                for h in range(4):
+                    nc.scalar.activation(
+                        out=junk[:],
+                        in_=state["sums", j][mi][:, HEAD * h : HEAD * (h + 1)],
+                        func=ACT.Square,
+                        accum_out=ssq[:, 4 * mi + h : 4 * mi + h + 1],
+                    )
+            mean = epi.tile([P, 8], F32, name="mean", tag="mean")
+            nc.scalar.activation(out=mean[:], in_=ssq[:], func=ACT.Copy, scale=1.0 / HEAD, bias=RMS_EPS)
+            state["mean", j] = mean
+
+        def factors(j):
+            c = j // 2
+            rstd = epi.tile([P, 8], F32, name="rstd", tag="rstd")
+            nc.gpsimd.tensor_tensor(out=rstd[:], in0=state["mean", j][:], in1=neg_half[:], op=ALU.pow)
+            fac = epi.tile([P, 2, 4], F32, name="fac", tag="fac")
+            nc.gpsimd.tensor_tensor(
+                out=fac[:],
+                in0=rstd[:].rearrange("p (m h) -> p m h", m=2),
+                in1=gain[:, 4 * c : 4 * c + 4].unsqueeze(1).to_broadcast([P, 2, 4]),
+                op=ALU.mult,
+            )
+            state["fac", j] = fac
+
+        def rope(j):
+            c = j // 2
+            prod = epi.tile([P, 8, 2, HEAD], F32, name="prod", tag="prod")
+            for mi in range(2):
+                m = 2 * (j % 2) + mi
+                for h in range(4):
+                    nc.vector.scalar_tensor_tensor(
+                        out=prod[:, 4 * mi + h, :, :],
+                        in0=state["sums", j][mi][:, HEAD * h : HEAD * (h + 1)].unsqueeze(1).to_broadcast([P, 2, HEAD]),
+                        scalar=state["fac", j][:, mi, h : h + 1],
+                        in1=tab[:, m, :, :],
+                        op0=ALU.mult,
+                        op1=ALU.mult,
+                    )
+            res = outp.tile([P, 8, HEAD], F32, name="res", tag="res")
+            nc.vector.tensor_tensor(
+                out=res[:, :, 0:HALF], in0=prod[:, :, 0, 0:HALF], in1=prod[:, :, 1, HALF:HEAD], op=ALU.add
+            )
+            nc.vector.tensor_tensor(
+                out=res[:, :, HALF:HEAD], in0=prod[:, :, 0, HALF:HEAD], in1=prod[:, :, 1, 0:HALF], op=ALU.add
+            )
+            nc.sync.dma_start(
+                out=dests[c].rearrange("(m p) n -> p m n", p=P)[:, 2 * (j % 2) : 2 * (j % 2) + 2, :],
+                in_=res[:].rearrange("p (m h) d -> p m (h d)", m=2),
+            )
+
+        def plain_out(j):
+            c = j // 2
+            for mi in range(2):
+                m = 2 * (j % 2) + mi
+                res = outp.tile([P, CHUNK], F32, name="res", tag="res")
+                nc.scalar.copy(out=res[:], in_=state["sums", j][mi][:])
+                nc.sync.dma_start(out=dests[c][P * m : P * (m + 1), :], in_=res[:])
+
+        for s in range(N_GROUPS + HEAD_UNITS):
+            j = s - HEAD_UNITS
+            e = j - 1
+            if s < N_UNITS:
+                transposes(s)
+            if 0 <= e < ROPE_GROUPS:
+                factors(e)
+            if s < N_UNITS:
+                copies(s)
+            if 0 <= j:
+                matmuls(j)
+            if 0 <= e < ROPE_GROUPS:
+                rope(e)
+            if s < N_UNITS:
+                quantise(s)
+            if 0 <= j < ROPE_GROUPS:
+                squares(j)
+            if j >= ROPE_GROUPS:
+                plain_out(j)

@@ -19,11 +19,12 @@ TOKENS = 512
 HEAD = 128
 HALF = 64
 CHUNK = 512
-N_UNITS = 14
-X_UNITS = 2
-HEAD_UNITS = 5
-N_GROUPS = 12
-ROPE_GROUPS = 10
+ROW_TILES = 28
+X_TILES = 4
+ROPE_CHUNKS = 5
+PRE_WARM = 6
+WARM_STEPS = 7
+V_COPY_STEPS = 10
 RMS_EPS = 1.1920929e-07
 PI = 3.141592653589793
 PI_HI = 102944.0 / 32768.0
@@ -36,39 +37,57 @@ FLOPS = 2 * TOKENS * K * 3072
 def tile_causalselfattention_pa_kernel(tc, x, w_qkv_tern, q_gain, out_0, out_1, out_2):
     nc = tc.nc
     x_rows = x.rearrange("b s k -> (b s) k")
-    row_tiles = [x_rows[P * i : P * (i + 1), :] for i in range(4)]
-    row_tiles.extend([w_qkv_tern[P * i : P * (i + 1), :] for i in range(24)])
+    row_tiles = [x_rows[P * i : P * (i + 1), :] for i in range(X_TILES)]
+    row_tiles.extend([w_qkv_tern[P * i : P * (i + 1), :] for i in range(ROW_TILES - X_TILES)])
     q_flat = out_0.rearrange("b s h d -> (b s) (h d)")
     dests = [q_flat[:, CHUNK * c : CHUNK * (c + 1)] for c in range(4)]
     dests.append(out_1.rearrange("b s h d -> (b s) (h d)"))
     dests.append(out_2.rearrange("b s h d -> (b s) (h d)"))
 
+    order = [0, 4, 5, 6, 7, 1, 2, 3]
+    order.extend(range(8, ROW_TILES))
+    pieces = []
+    for m in range(4):
+        pieces.append((0, m, (0, 1)))
+        pieces.append((0, m, (2, 3)))
+    for c in range(1, 6):
+        for m in range(4):
+            pieces.append((c, m, (0, 1, 2, 3)))
+
     with ExitStack() as ctx:
         const = ctx.enter_context(tc.tile_pool(name="const", bufs=1))
-        rawp = ctx.enter_context(tc.tile_pool(name="rawp", bufs=28))
-        grpp = ctx.enter_context(tc.tile_pool(name="grpp", bufs=8))
+        rawp = ctx.enter_context(tc.tile_pool(name="rawp", bufs=ROW_TILES))
+        grpp = ctx.enter_context(tc.tile_pool(name="grpp", bufs=6))
         codep = ctx.enter_context(tc.tile_pool(name="codep", bufs=3))
-        epi = ctx.enter_context(tc.tile_pool(name="epi", bufs=2))
-        outp = ctx.enter_context(tc.tile_pool(name="outp", bufs=6))
+        epi = ctx.enter_context(tc.tile_pool(name="epi", bufs=3))
+        outp = ctx.enter_context(tc.tile_pool(name="outp", bufs=8))
         tps = ctx.enter_context(tc.psum_pool(name="tps", bufs=4))
         accs = ctx.enter_context(tc.psum_pool(name="accs", bufs=4))
         ctx.enter_context(tc.manual_schedule())
 
         gain_bf = const.tile([P, 16], BF16, name="gain_bf")
-        raws = []
-        for i in range(28):
+        raws = {}
+        for i in range(ROW_TILES):
             raw = rawp.tile([P, K], BF16, name="raw", tag="raw")
-            nc.sync.dma_start(out=raw[:], in_=row_tiles[i])
-            raws.append(raw)
-            if i == 2 * HEAD_UNITS - 1:
+            nc.sync.dma_start(out=raw[:], in_=row_tiles[order[i]])
+            raws[i] = raw
+            if i == 11:
                 nc.sync.dma_start(out=gain_bf[:], in_=q_gain.partition_broadcast(P))
+
+        warm = const.tile([P, CHUNK], BF16, name="warm")
+        nc.vector.memset(warm[:], 0.0)
+        idle_sum = accs.tile([P, CHUNK], F32, name="acc", tag="acc")
+
+        def keep_warm():
+            nc.tensor.matmul(out=idle_sum[:], lhsT=warm[:, 0:P], rhs=warm[:], start=True, stop=True)
+
+        for i in range(PRE_WARM):
+            keep_warm()
 
         t_int = const.tile([P, 4], I32, name="t_int")
         nc.gpsimd.iota(t_int[:], pattern=[[P, 4]], base=0, channel_multiplier=1)
         ident = const.tile([P, P], F32, name="ident")
         make_identity(nc, ident[:])
-        neg_half = const.tile([P, 8], F32, name="neg_half")
-        nc.gpsimd.memset(neg_half[:], -0.5)
         gain = const.tile([P, 20], F32, name="gain")
         nc.gpsimd.memset(gain[:], 1.0)
 
@@ -101,6 +120,8 @@ def tile_causalselfattention_pa_kernel(tc, x, w_qkv_tern, q_gain, out_0, out_1, 
         nc.scalar.activation(out=sin_a[:], in_=red[:], func=ACT.Sin)
         sin_b = const.tile([P, 4, HALF], F32, name="sin_b")
         nc.scalar.activation(out=sin_b[:], in_=red[:], func=ACT.Sin, bias=-PI / 4.0)
+        first_rstd = const.tile([P, 1], F32, name="first_rstd")
+        nc.scalar.activation(out=first_rstd[:], in_=gain[:, 16:17], func=ACT.Abs_reciprocal_sqrt)
         sq_a = const.tile([P, 4, HALF], F32, name="sq_a")
         nc.gpsimd.tensor_tensor(out=sq_a[:], in0=sin_a[:], in1=sin_a[:], op=ALU.mult)
         sq_b = const.tile([P, 4, HALF], F32, name="sq_b")
@@ -123,152 +144,151 @@ def tile_causalselfattention_pa_kernel(tc, x, w_qkv_tern, q_gain, out_0, out_1, 
 
         state = {}
 
-        def transposes(s):
-            banks = [tps.tile([P, 2, 2 * P], F32, name="tp", tag="tp") for g in range(PASSES)]
-            for r in range(2):
-                words = raws[2 * s + r][:].bitcast(F32)
-                for g in range(PASSES):
-                    for u in range(2):
-                        nc.tensor.transpose(
-                            banks[g][:, u, P * r : P * (r + 1)],
-                            words[:, 256 * g + u : 256 * (g + 1) : 2],
-                            ident[:],
-                        )
+        def transposes(t):
+            banks = [tps.tile([P, 2, 2, P], F32, name="tp", tag="tp") for b in range(2)]
+            words = raws[t][:].bitcast(F32)
+            for g in range(PASSES):
+                for u in range(2):
+                    nc.tensor.transpose(
+                        banks[g // 2][:, g % 2, u, :], words[:, 256 * g + u : 256 * (g + 1) : 2], ident[:]
+                    )
+                if t < WARM_STEPS and g % 2 == 1:
+                    keep_warm()
             state["banks"] = banks
 
-        def copies(s):
+        def copies(t):
             groups = []
-            for g in range(PASSES):
+            for b in range(2):
                 grp = grpp.tile([P, 8 * P], BF16, name="grp", tag="grp", align_bytes=64)
-                dst = grp[:].bitcast(F32).rearrange("p (n u) -> p n u", u=2)
-                src = state["banks"][g][:].rearrange("p u n -> p n u")
-                if s < HEAD_UNITS and g == PASSES - 1:
+                dst = grp[:].bitcast(F32).rearrange("p (g c u) -> p g c u", g=2, u=2)
+                src = state["banks"][b][:].rearrange("p g u c -> p g c u")
+                if t < V_COPY_STEPS and b == 1:
                     nc.vector.tensor_copy(out=dst, in_=src)
                 else:
                     nc.scalar.copy(out=dst, in_=src)
                 groups.append(grp)
-            state["groups"] = groups
+            state["groups", t] = groups
 
-        def quantise(s):
-            if s < X_UNITS:
-                codes, scales, lo = x_codes, x_scales, 2 * P * s
+        def quantise(t):
+            tile_no = order[t]
+            if tile_no < X_TILES:
+                codes, scales, lo = x_codes, x_scales, P * tile_no
             else:
-                if (s - X_UNITS) % 2 == 0:
-                    state["w_codes", (s - X_UNITS) // 2] = codep.tile(
+                c = (tile_no - X_TILES) // 4
+                lo = P * ((tile_no - X_TILES) % 4)
+                if lo == 0:
+                    state["w_codes", c] = codep.tile(
                         [P, PASSES, CHUNK], U32, name="w_codes", tag="w_codes", align_bytes=64
                     )
-                    state["w_scales", (s - X_UNITS) // 2] = codep.tile(
+                    state["w_scales", c] = codep.tile(
                         [P, PASSES, CHUNK], U8, name="w_scales", tag="w_scales", align_bytes=64
                     )
-                codes = state["w_codes", (s - X_UNITS) // 2]
-                scales = state["w_scales", (s - X_UNITS) // 2]
-                lo = 2 * P * ((s - X_UNITS) % 2)
+                codes, scales = state["w_codes", c], state["w_scales", c]
             for g in range(PASSES):
                 nc.vector.quantize_mx(
-                    out=codes[:, g, lo : lo + 2 * P].bitcast(E5X4),
-                    scales=scales[:, g, lo : lo + 2 * P],
-                    in_=state["groups"][g][:],
+                    out=codes[:, g, lo : lo + P].bitcast(E5X4),
+                    scales=scales[:, g, lo : lo + P],
+                    in_=state["groups", t][g // 2][:, 4 * P * (g % 2) : 4 * P * (g % 2 + 1)],
                 )
 
-        def matmuls(j):
-            c = j // 2
-            sums = []
-            for mi in range(2):
-                m = 2 * (j % 2) + mi
-                if j < ROPE_GROUPS:
-                    acc = accs.tile([P, CHUNK], F32, name="acc", tag="acc")
+        def matmuls(c, m, passes):
+            if passes[0] == 0:
+                if c < ROPE_CHUNKS:
+                    state["sum", c, m] = accs.tile([P, CHUNK], F32, name="acc", tag="acc")
                 else:
-                    acc = tps.tile([P, CHUNK], F32, name="tp", tag="tp")
-                for g in range(PASSES):
-                    nc.tensor.matmul_mx(
-                        out=acc[:],
-                        lhsT=x_codes[:, g, P * m : P * (m + 1)].bitcast(E5X4),
-                        lhsT_scale=x_scales[:, g, P * m : P * (m + 1)],
-                        rhs=state["w_codes", c][:, g, :].bitcast(E5X4),
-                        rhs_scale=state["w_scales", c][:, g, :],
-                        start=(g == 0),
-                        stop=(g == PASSES - 1),
-                    )
-                sums.append(acc)
-            state["sums", j] = sums
+                    state["sum", c, m] = tps.tile([P, CHUNK], F32, name="tp", tag="tp")
+            for g in passes:
+                nc.tensor.matmul_mx(
+                    out=state["sum", c, m][:],
+                    lhsT=x_codes[:, g, P * m : P * (m + 1)].bitcast(E5X4),
+                    lhsT_scale=x_scales[:, g, P * m : P * (m + 1)],
+                    rhs=state["w_codes", c][:, g, :].bitcast(E5X4),
+                    rhs_scale=state["w_scales", c][:, g, :],
+                    start=(g == 0),
+                    stop=(g == PASSES - 1),
+                )
 
-        def squares(j):
-            ssq = epi.tile([P, 8], F32, name="ssq", tag="ssq")
-            for mi in range(2):
-                for h in range(4):
-                    nc.scalar.activation(
-                        out=junk[:],
-                        in_=state["sums", j][mi][:, HEAD * h : HEAD * (h + 1)],
-                        func=ACT.Square,
-                        accum_out=ssq[:, 4 * mi + h : 4 * mi + h + 1],
-                    )
-            mean = epi.tile([P, 8], F32, name="mean", tag="mean")
-            nc.scalar.activation(out=mean[:], in_=ssq[:], func=ACT.Copy, scale=1.0 / HEAD, bias=RMS_EPS)
-            state["mean", j] = mean
+        def squares(c, m):
+            if m % 2 == 0:
+                state["ssq", c] = epi.tile([P, 8], F32, name="ssq", tag="ssq")
+            ssq = state["ssq", c]
+            for h in range(4):
+                col = 4 * (m % 2) + h
+                nc.scalar.activation(
+                    out=junk[:],
+                    in_=state["sum", c, m][:, HEAD * h : HEAD * (h + 1)],
+                    func=ACT.Square,
+                    accum_out=ssq[:, col : col + 1],
+                )
+            if m % 2 == 1:
+                rstd = epi.tile([P, 8], F32, name="rstd", tag="rstd")
+                nc.scalar.activation(
+                    out=rstd[:], in_=ssq[:], func=ACT.Abs_reciprocal_sqrt, scale=1.0 / HEAD, bias=RMS_EPS
+                )
+                state["rstd", c, m // 2] = rstd
 
-        def factors(j):
-            c = j // 2
-            rstd = epi.tile([P, 8], F32, name="rstd", tag="rstd")
-            nc.gpsimd.tensor_tensor(out=rstd[:], in0=state["mean", j][:], in1=neg_half[:], op=ALU.pow)
+        def factors(c, pair):
             fac = epi.tile([P, 2, 4], F32, name="fac", tag="fac")
-            nc.gpsimd.tensor_tensor(
+            nc.vector.tensor_tensor(
                 out=fac[:],
-                in0=rstd[:].rearrange("p (m h) -> p m h", m=2),
+                in0=state["rstd", c, pair][:].rearrange("p (m h) -> p m h", m=2),
                 in1=gain[:, 4 * c : 4 * c + 4].unsqueeze(1).to_broadcast([P, 2, 4]),
                 op=ALU.mult,
             )
-            state["fac", j] = fac
+            state["fac", c, pair] = fac
 
-        def rope(j):
-            c = j // 2
-            prod = epi.tile([P, 8, 2, HEAD], F32, name="prod", tag="prod")
-            for mi in range(2):
-                m = 2 * (j % 2) + mi
-                for h in range(4):
-                    nc.vector.scalar_tensor_tensor(
-                        out=prod[:, 4 * mi + h, :, :],
-                        in0=state["sums", j][mi][:, HEAD * h : HEAD * (h + 1)].unsqueeze(1).to_broadcast([P, 2, HEAD]),
-                        scalar=state["fac", j][:, mi, h : h + 1],
-                        in1=tab[:, m, :, :],
-                        op0=ALU.mult,
-                        op1=ALU.mult,
-                    )
-            res = outp.tile([P, 8, HEAD], F32, name="res", tag="res")
+        def rope(c, m):
+            prod = epi.tile([P, 4, 2, HEAD], F32, name="prod", tag="prod")
+            for h in range(4):
+                nc.vector.scalar_tensor_tensor(
+                    out=prod[:, h, :, :],
+                    in0=state["sum", c, m][:, HEAD * h : HEAD * (h + 1)].unsqueeze(1).to_broadcast([P, 2, HEAD]),
+                    scalar=state["fac", c, m // 2][:, m % 2, h : h + 1],
+                    in1=tab[:, m, :, :],
+                    op0=ALU.mult,
+                    op1=ALU.mult,
+                )
+            res = outp.tile([P, 4, HEAD], F32, name="res", tag="res")
             nc.vector.tensor_tensor(
                 out=res[:, :, 0:HALF], in0=prod[:, :, 0, 0:HALF], in1=prod[:, :, 1, HALF:HEAD], op=ALU.add
             )
             nc.vector.tensor_tensor(
                 out=res[:, :, HALF:HEAD], in0=prod[:, :, 0, HALF:HEAD], in1=prod[:, :, 1, 0:HALF], op=ALU.add
             )
-            nc.sync.dma_start(
-                out=dests[c].rearrange("(m p) n -> p m n", p=P)[:, 2 * (j % 2) : 2 * (j % 2) + 2, :],
-                in_=res[:].rearrange("p (m h) d -> p m (h d)", m=2),
-            )
+            nc.sync.dma_start(out=dests[c][P * m : P * (m + 1), :], in_=res[:].rearrange("p h d -> p (h d)"))
 
-        def plain_out(j):
-            c = j // 2
-            for mi in range(2):
-                m = 2 * (j % 2) + mi
-                res = outp.tile([P, CHUNK], F32, name="res", tag="res")
-                nc.scalar.copy(out=res[:], in_=state["sums", j][mi][:])
-                nc.sync.dma_start(out=dests[c][P * m : P * (m + 1), :], in_=res[:])
+        def plain_out(c, m):
+            res = outp.tile([P, CHUNK], F32, name="res", tag="res")
+            nc.scalar.copy(out=res[:], in_=state["sum", c, m][:])
+            nc.sync.dma_start(out=dests[c][P * m : P * (m + 1), :], in_=res[:])
 
-        for s in range(N_GROUPS + HEAD_UNITS):
-            j = s - HEAD_UNITS
-            e = j - 1
-            if s < N_UNITS:
-                transposes(s)
-            if 0 <= e < ROPE_GROUPS:
-                factors(e)
-            if s < N_UNITS:
-                copies(s)
-            if 0 <= j:
-                matmuls(j)
-            if 0 <= e < ROPE_GROUPS:
-                rope(e)
-            if s < N_UNITS:
-                quantise(s)
-            if 0 <= j < ROPE_GROUPS:
-                squares(j)
-            if j >= ROPE_GROUPS:
-                plain_out(j)
+        factor_at = {}
+        rope_at = {}
+        for t in range(WARM_STEPS + len(pieces) + 3):
+            q = t - WARM_STEPS
+            closed = None
+            if 0 <= q < len(pieces):
+                c, m, passes = pieces[q]
+                matmuls(c, m, passes)
+                if passes[-1] == PASSES - 1:
+                    closed = (c, m)
+            if t < ROW_TILES:
+                transposes(t)
+            if closed is not None:
+                c, m = closed
+                if c < ROPE_CHUNKS:
+                    squares(c, m)
+                    if m % 2 == 1:
+                        factor_at[t + 1] = (c, m // 2)
+                        rope_at[t + 1] = (c, m - 1)
+                        rope_at[t + 2] = (c, m)
+                else:
+                    plain_out(c, m)
+            if 1 <= t <= ROW_TILES:
+                quantise(t - 1)
+            if t in factor_at:
+                factors(factor_at[t][0], factor_at[t][1])
+            if t in rope_at:
+                rope(rope_at[t][0], rope_at[t][1])
+            if t < ROW_TILES:
+                copies(t)

@@ -19,11 +19,10 @@ TOKENS = 512
 HEAD = 128
 HALF = 64
 CHUNK = 512
-ROW_TILES = 28
-X_TILES = 4
+BLOCKS = 7
+STEPS_T = 4 * BLOCKS
 ROPE_CHUNKS = 5
 PRE_WARM = 6
-WARM_STEPS = 7
 V_COPY_STEPS = 10
 RMS_EPS = 1.1920929e-07
 PI = 3.141592653589793
@@ -36,53 +35,60 @@ FLOPS = 2 * TOKENS * K * 3072
 
 def tile_causalselfattention_pa_kernel(tc, x, w_qkv_tern, q_gain, out_0, out_1, out_2):
     nc = tc.nc
-    x_rows = x.rearrange("b s k -> (b s) k")
-    row_tiles = [x_rows[P * i : P * (i + 1), :] for i in range(X_TILES)]
-    row_tiles.extend([w_qkv_tern[P * i : P * (i + 1), :] for i in range(ROW_TILES - X_TILES)])
+    blocks = [x.rearrange("b (r p) k -> p (b r) k", p=P)]
+    for c in range(BLOCKS - 1):
+        blocks.append(w_qkv_tern[CHUNK * c : CHUNK * (c + 1), :].rearrange("(r p) k -> p r k", p=P))
     q_flat = out_0.rearrange("b s h d -> (b s) (h d)")
     dests = [q_flat[:, CHUNK * c : CHUNK * (c + 1)] for c in range(4)]
     dests.append(out_1.rearrange("b s h d -> (b s) (h d)"))
     dests.append(out_2.rearrange("b s h d -> (b s) (h d)"))
 
-    order = [0, 4, 5, 6, 7, 1, 2, 3]
-    order.extend(range(8, ROW_TILES))
-    pieces = []
+    order = []
+    for g in range(PASSES):
+        order.append((0, g))
+        order.append((1, g))
+    for b in range(2, BLOCKS):
+        for g in range(PASSES):
+            order.append((b, g))
+    work = {}
+    for i in range(8):
+        work[4 + i] = [(0, 2 * (i % 2), i // 2), (0, 2 * (i % 2) + 1, i // 2)]
+    for c in range(1, ROPE_CHUNKS):
+        for i in range(4):
+            work[9 + 4 * c + i] = [(c, 2 * (i // 2) + mi, 2 * (i % 2) + gi) for mi in range(2) for gi in range(2)]
     for m in range(4):
-        pieces.append((0, m, (0, 1)))
-        pieces.append((0, m, (2, 3)))
-    for c in range(1, 6):
-        for m in range(4):
-            pieces.append((c, m, (0, 1, 2, 3)))
+        work[9 + 4 * ROPE_CHUNKS + m] = [(ROPE_CHUNKS, m, g) for g in range(PASSES)]
+    last_step = 9 + 4 * ROPE_CHUNKS + 3
 
     with ExitStack() as ctx:
         const = ctx.enter_context(tc.tile_pool(name="const", bufs=1))
-        rawp = ctx.enter_context(tc.tile_pool(name="rawp", bufs=ROW_TILES))
-        grpp = ctx.enter_context(tc.tile_pool(name="grpp", bufs=6))
+        rawp = ctx.enter_context(tc.tile_pool(name="rawp", bufs=8))
+        grpp = ctx.enter_context(tc.tile_pool(name="grpp", bufs=4))
         codep = ctx.enter_context(tc.tile_pool(name="codep", bufs=3))
-        epi = ctx.enter_context(tc.tile_pool(name="epi", bufs=3))
-        outp = ctx.enter_context(tc.tile_pool(name="outp", bufs=8))
+        epi = ctx.enter_context(tc.tile_pool(name="epi", bufs=2))
+        outp = ctx.enter_context(tc.tile_pool(name="outp", bufs=5))
         tps = ctx.enter_context(tc.psum_pool(name="tps", bufs=4))
         accs = ctx.enter_context(tc.psum_pool(name="accs", bufs=4))
         ctx.enter_context(tc.manual_schedule())
 
         gain_bf = const.tile([P, 16], BF16, name="gain_bf")
-        raws = {}
-        for i in range(ROW_TILES):
-            raw = rawp.tile([P, K], BF16, name="raw", tag="raw")
-            nc.sync.dma_start(out=raw[:], in_=row_tiles[order[i]])
-            raws[i] = raw
-            if i == 11:
+        raws = []
+        for t in range(STEPS_T):
+            b, g = order[t]
+            if b < 2:
+                raw = rawp.tile([P, 4, CHUNK], BF16, name="raw", tag="raw")
+                nc.sync.dma_start(out=raw[:], in_=blocks[b][:, :, CHUNK * g : CHUNK * (g + 1)])
+                raws.append(raw[:])
+            elif g % 2 == 0:
+                raw2 = rawp.tile([P, 4, 2 * CHUNK], BF16, name="raw2", tag="raw2", bufs=10)
+                nc.sync.dma_start(out=raw2[:], in_=blocks[b][:, :, CHUNK * g : CHUNK * (g + 2)])
+                raws.append(raw2[:, :, 0:CHUNK])
+                raws.append(raw2[:, :, CHUNK : 2 * CHUNK])
+            if t == 11:
                 nc.sync.dma_start(out=gain_bf[:], in_=q_gain.partition_broadcast(P))
 
         warm = const.tile([P, CHUNK], BF16, name="warm")
         nc.vector.memset(warm[:], 0.0)
-        idle_sum = accs.tile([P, CHUNK], F32, name="acc", tag="acc")
-
-        def keep_warm():
-            nc.tensor.matmul(out=idle_sum[:], lhsT=warm[:, 0:P], rhs=warm[:], start=True, stop=True)
-
-        for i in range(PRE_WARM):
-            keep_warm()
 
         t_int = const.tile([P, 4], I32, name="t_int")
         nc.gpsimd.iota(t_int[:], pattern=[[P, 4]], base=0, channel_multiplier=1)
@@ -144,69 +150,65 @@ def tile_causalselfattention_pa_kernel(tc, x, w_qkv_tern, q_gain, out_0, out_1, 
 
         state = {}
 
+        def keep_warm(bank):
+            nc.tensor.matmul(
+                out=bank[:].rearrange("p r u c -> p (r u c)"), lhsT=warm[:, 0:P], rhs=warm[:], start=True, stop=True
+            )
+
         def transposes(t):
             banks = [tps.tile([P, 2, 2, P], F32, name="tp", tag="tp") for b in range(2)]
-            words = raws[t][:].bitcast(F32)
-            for g in range(PASSES):
+            if t == 0:
+                for i in range(PRE_WARM):
+                    keep_warm(banks[0])
+            for r in range(4):
+                if t not in work and r % 2 == 0:
+                    keep_warm(banks[r // 2])
+                words = raws[t][:, r, :].bitcast(F32)
                 for u in range(2):
-                    nc.tensor.transpose(
-                        banks[g // 2][:, g % 2, u, :], words[:, 256 * g + u : 256 * (g + 1) : 2], ident[:]
-                    )
-                if t < WARM_STEPS and g % 2 == 1:
-                    keep_warm()
+                    nc.tensor.transpose(banks[r // 2][:, r % 2, u, :], words[:, u : 2 * P : 2], ident[:])
             state["banks"] = banks
 
         def copies(t):
-            groups = []
+            grp = grpp.tile([P, 16 * P], BF16, name="grp", tag="grp", align_bytes=64)
             for b in range(2):
-                grp = grpp.tile([P, 8 * P], BF16, name="grp", tag="grp", align_bytes=64)
-                dst = grp[:].bitcast(F32).rearrange("p (g c u) -> p g c u", g=2, u=2)
-                src = state["banks"][b][:].rearrange("p g u c -> p g c u")
+                dst = grp[:, 8 * P * b : 8 * P * (b + 1)].bitcast(F32).rearrange("p (r c u) -> p r c u", r=2, u=2)
+                src = state["banks"][b][:].rearrange("p r u c -> p r c u")
                 if t < V_COPY_STEPS and b == 1:
                     nc.vector.tensor_copy(out=dst, in_=src)
                 else:
                     nc.scalar.copy(out=dst, in_=src)
-                groups.append(grp)
-            state["groups", t] = groups
+            state["grp", t] = grp
 
         def quantise(t):
-            tile_no = order[t]
-            if tile_no < X_TILES:
-                codes, scales, lo = x_codes, x_scales, P * tile_no
+            b, g = order[t]
+            if b == 0:
+                codes, scales = x_codes, x_scales
             else:
-                c = (tile_no - X_TILES) // 4
-                lo = P * ((tile_no - X_TILES) % 4)
-                if lo == 0:
-                    state["w_codes", c] = codep.tile(
+                if g == 0:
+                    state["w_codes", b - 1] = codep.tile(
                         [P, PASSES, CHUNK], U32, name="w_codes", tag="w_codes", align_bytes=64
                     )
-                    state["w_scales", c] = codep.tile(
+                    state["w_scales", b - 1] = codep.tile(
                         [P, PASSES, CHUNK], U8, name="w_scales", tag="w_scales", align_bytes=64
                     )
-                codes, scales = state["w_codes", c], state["w_scales", c]
-            for g in range(PASSES):
-                nc.vector.quantize_mx(
-                    out=codes[:, g, lo : lo + P].bitcast(E5X4),
-                    scales=scales[:, g, lo : lo + P],
-                    in_=state["groups", t][g // 2][:, 4 * P * (g % 2) : 4 * P * (g % 2 + 1)],
-                )
+                codes, scales = state["w_codes", b - 1], state["w_scales", b - 1]
+            nc.vector.quantize_mx(out=codes[:, g, :].bitcast(E5X4), scales=scales[:, g, :], in_=state["grp", t][:])
 
-        def matmuls(c, m, passes):
-            if passes[0] == 0:
+        def matmul(c, m, g):
+            if g == 0:
                 if c < ROPE_CHUNKS:
                     state["sum", c, m] = accs.tile([P, CHUNK], F32, name="acc", tag="acc")
                 else:
                     state["sum", c, m] = tps.tile([P, CHUNK], F32, name="tp", tag="tp")
-            for g in passes:
-                nc.tensor.matmul_mx(
-                    out=state["sum", c, m][:],
-                    lhsT=x_codes[:, g, P * m : P * (m + 1)].bitcast(E5X4),
-                    lhsT_scale=x_scales[:, g, P * m : P * (m + 1)],
-                    rhs=state["w_codes", c][:, g, :].bitcast(E5X4),
-                    rhs_scale=state["w_scales", c][:, g, :],
-                    start=(g == 0),
-                    stop=(g == PASSES - 1),
-                )
+            nc.tensor.matmul_mx(
+                out=state["sum", c, m][:],
+                lhsT=x_codes[:, g, P * m : P * (m + 1)].bitcast(E5X4),
+                lhsT_scale=x_scales[:, g, P * m : P * (m + 1)],
+                rhs=state["w_codes", c][:, g, :].bitcast(E5X4),
+                rhs_scale=state["w_scales", c][:, g, :],
+                start=(g == 0),
+                stop=(g == PASSES - 1),
+            )
 
         def squares(c, m):
             if m % 2 == 0:
@@ -227,68 +229,65 @@ def tile_causalselfattention_pa_kernel(tc, x, w_qkv_tern, q_gain, out_0, out_1, 
                 )
                 state["rstd", c, m // 2] = rstd
 
-        def factors(c, pair):
-            fac = epi.tile([P, 2, 4], F32, name="fac", tag="fac")
-            nc.vector.tensor_tensor(
-                out=fac[:],
-                in0=state["rstd", c, pair][:].rearrange("p (m h) -> p m h", m=2),
-                in1=gain[:, 4 * c : 4 * c + 4].unsqueeze(1).to_broadcast([P, 2, 4]),
-                op=ALU.mult,
-            )
-            state["fac", c, pair] = fac
-
         def rope(c, m):
-            prod = epi.tile([P, 4, 2, HEAD], F32, name="prod", tag="prod")
+            pair = m // 2
+            if m % 2 == 0:
+                fac = epi.tile([P, 2, 4], F32, name="fac", tag="fac")
+                nc.vector.tensor_tensor(
+                    out=fac[:],
+                    in0=state["rstd", c, pair][:].rearrange("p (m h) -> p m h", m=2),
+                    in1=gain[:, 4 * c : 4 * c + 4].unsqueeze(1).to_broadcast([P, 2, 4]),
+                    op=ALU.mult,
+                )
+                state["fac"] = fac
+                state["prod"] = epi.tile([P, 8, 2, HEAD], F32, name="prod", tag="prod")
+            prod = state["prod"]
             for h in range(4):
                 nc.vector.scalar_tensor_tensor(
-                    out=prod[:, h, :, :],
+                    out=prod[:, 4 * (m % 2) + h, :, :],
                     in0=state["sum", c, m][:, HEAD * h : HEAD * (h + 1)].unsqueeze(1).to_broadcast([P, 2, HEAD]),
-                    scalar=state["fac", c, m // 2][:, m % 2, h : h + 1],
+                    scalar=state["fac"][:, m % 2, h : h + 1],
                     in1=tab[:, m, :, :],
                     op0=ALU.mult,
                     op1=ALU.mult,
                 )
-            res = outp.tile([P, 4, HEAD], F32, name="res", tag="res")
-            nc.vector.tensor_tensor(
-                out=res[:, :, 0:HALF], in0=prod[:, :, 0, 0:HALF], in1=prod[:, :, 1, HALF:HEAD], op=ALU.add
-            )
-            nc.vector.tensor_tensor(
-                out=res[:, :, HALF:HEAD], in0=prod[:, :, 0, HALF:HEAD], in1=prod[:, :, 1, 0:HALF], op=ALU.add
-            )
-            nc.sync.dma_start(out=dests[c][P * m : P * (m + 1), :], in_=res[:].rearrange("p h d -> p (h d)"))
+            if m % 2 == 1:
+                res = outp.tile([P, 8, HEAD], F32, name="res", tag="res")
+                nc.vector.tensor_tensor(
+                    out=res[:, :, 0:HALF], in0=prod[:, :, 0, 0:HALF], in1=prod[:, :, 1, HALF:HEAD], op=ALU.add
+                )
+                nc.vector.tensor_tensor(
+                    out=res[:, :, HALF:HEAD], in0=prod[:, :, 0, HALF:HEAD], in1=prod[:, :, 1, 0:HALF], op=ALU.add
+                )
+                nc.sync.dma_start(
+                    out=dests[c].rearrange("(m p) n -> p m n", p=P)[:, 2 * pair : 2 * pair + 2, :],
+                    in_=res[:].rearrange("p (m h) d -> p m (h d)", m=2),
+                )
 
         def plain_out(c, m):
             res = outp.tile([P, CHUNK], F32, name="res", tag="res")
             nc.scalar.copy(out=res[:], in_=state["sum", c, m][:])
             nc.sync.dma_start(out=dests[c][P * m : P * (m + 1), :], in_=res[:])
 
-        factor_at = {}
-        rope_at = {}
-        for t in range(WARM_STEPS + len(pieces) + 3):
-            q = t - WARM_STEPS
-            closed = None
-            if 0 <= q < len(pieces):
-                c, m, passes = pieces[q]
-                matmuls(c, m, passes)
-                if passes[-1] == PASSES - 1:
-                    closed = (c, m)
-            if t < ROW_TILES:
+        waiting = []
+        for t in range(last_step + 4):
+            ready = len(waiting)
+            for c, m, g in work.get(t, []):
+                matmul(c, m, g)
+            if t < STEPS_T:
                 transposes(t)
-            if closed is not None:
-                c, m = closed
-                if c < ROPE_CHUNKS:
-                    squares(c, m)
-                    if m % 2 == 1:
-                        factor_at[t + 1] = (c, m // 2)
-                        rope_at[t + 1] = (c, m - 1)
-                        rope_at[t + 2] = (c, m)
-                else:
-                    plain_out(c, m)
-            if 1 <= t <= ROW_TILES:
+            for c, m, g in work.get(t, []):
+                if g == PASSES - 1:
+                    if c < ROPE_CHUNKS:
+                        squares(c, m)
+                        waiting.append((c, m))
+                    else:
+                        plain_out(c, m)
+            if ready > 0 and (ready > 1 or waiting[0][1] % 2 == 1):
+                c, m = waiting[0]
+                waiting.remove(waiting[0])
+                rope(c, m)
+            if 1 <= t <= STEPS_T:
                 quantise(t - 1)
-            if t in factor_at:
-                factors(factor_at[t][0], factor_at[t][1])
-            if t in rope_at:
-                rope(rope_at[t][0], rope_at[t][1])
-            if t < ROW_TILES:
+            if t < STEPS_T:
                 copies(t)

@@ -19,11 +19,13 @@ TOKENS = 512
 HEAD = 128
 HALF = 64
 CHUNK = 512
-BLOCKS = 7
-STEPS_T = 4 * BLOCKS
+ROW_TILES = 28
+X_TILES = 4
 ROPE_CHUNKS = 5
 PRE_WARM = 6
-V_COPY_STEPS = 10
+WARM_STEPS = 7
+V_COPY_STEPS = 2
+SORTED_STEPS = 10
 RMS_EPS = 1.1920929e-07
 PI = 3.141592653589793
 PI_HI = 102944.0 / 32768.0
@@ -35,60 +37,54 @@ FLOPS = 2 * TOKENS * K * 3072
 
 def tile_causalselfattention_pa_kernel(tc, x, w_qkv_tern, q_gain, out_0, out_1, out_2):
     nc = tc.nc
-    blocks = [x.rearrange("b (r p) k -> p (b r) k", p=P)]
-    for c in range(BLOCKS - 1):
-        blocks.append(w_qkv_tern[CHUNK * c : CHUNK * (c + 1), :].rearrange("(r p) k -> p r k", p=P))
+    x_rows = x.rearrange("b s k -> (b s) k")
+    row_tiles = [x_rows[P * i : P * (i + 1), :] for i in range(X_TILES)]
+    row_tiles.extend([w_qkv_tern[P * i : P * (i + 1), :] for i in range(ROW_TILES - X_TILES)])
     q_flat = out_0.rearrange("b s h d -> (b s) (h d)")
     dests = [q_flat[:, CHUNK * c : CHUNK * (c + 1)] for c in range(4)]
     dests.append(out_1.rearrange("b s h d -> (b s) (h d)"))
     dests.append(out_2.rearrange("b s h d -> (b s) (h d)"))
 
-    order = []
-    for g in range(PASSES):
-        order.append((0, g))
-        order.append((1, g))
-    for b in range(2, BLOCKS):
-        for g in range(PASSES):
-            order.append((b, g))
-    work = {}
-    for i in range(8):
-        work[4 + i] = [(0, 2 * (i % 2), i // 2), (0, 2 * (i % 2) + 1, i // 2)]
-    for c in range(1, ROPE_CHUNKS):
-        for i in range(4):
-            work[9 + 4 * c + i] = [(c, 2 * (i // 2) + mi, 2 * (i % 2) + gi) for mi in range(2) for gi in range(2)]
+    order = [0, 4, 5, 6, 7, 1, 2, 3]
+    order.extend(range(8, ROW_TILES))
+    pieces = []
     for m in range(4):
-        work[9 + 4 * ROPE_CHUNKS + m] = [(ROPE_CHUNKS, m, g) for g in range(PASSES)]
-    last_step = 9 + 4 * ROPE_CHUNKS + 3
+        pieces.append((0, m, (0, 1)))
+        pieces.append((0, m, (2, 3)))
+    for c in range(1, 6):
+        for m in range(4):
+            pieces.append((c, m, (0, 1, 2, 3)))
 
     with ExitStack() as ctx:
         const = ctx.enter_context(tc.tile_pool(name="const", bufs=1))
-        rawp = ctx.enter_context(tc.tile_pool(name="rawp", bufs=8))
-        grpp = ctx.enter_context(tc.tile_pool(name="grpp", bufs=4))
+        rawp = ctx.enter_context(tc.tile_pool(name="rawp", bufs=ROW_TILES))
+        sortp = ctx.enter_context(tc.tile_pool(name="sortp", bufs=3))
+        grpp = ctx.enter_context(tc.tile_pool(name="grpp", bufs=6))
         codep = ctx.enter_context(tc.tile_pool(name="codep", bufs=3))
-        epi = ctx.enter_context(tc.tile_pool(name="epi", bufs=2))
-        outp = ctx.enter_context(tc.tile_pool(name="outp", bufs=5))
+        epi = ctx.enter_context(tc.tile_pool(name="epi", bufs=3))
+        outp = ctx.enter_context(tc.tile_pool(name="outp", bufs=8))
         tps = ctx.enter_context(tc.psum_pool(name="tps", bufs=4))
         accs = ctx.enter_context(tc.psum_pool(name="accs", bufs=4))
         ctx.enter_context(tc.manual_schedule())
 
         gain_bf = const.tile([P, 16], BF16, name="gain_bf")
-        raws = []
-        for t in range(STEPS_T):
-            b, g = order[t]
-            if b < 2:
-                raw = rawp.tile([P, 4, CHUNK], BF16, name="raw", tag="raw")
-                nc.sync.dma_start(out=raw[:], in_=blocks[b][:, :, CHUNK * g : CHUNK * (g + 1)])
-                raws.append(raw[:])
-            elif g % 2 == 0:
-                raw2 = rawp.tile([P, 4, 2 * CHUNK], BF16, name="raw2", tag="raw2", bufs=10)
-                nc.sync.dma_start(out=raw2[:], in_=blocks[b][:, :, CHUNK * g : CHUNK * (g + 2)])
-                raws.append(raw2[:, :, 0:CHUNK])
-                raws.append(raw2[:, :, CHUNK : 2 * CHUNK])
-            if t == 11:
+        raws = {}
+        for i in range(ROW_TILES):
+            raw = rawp.tile([P, K], BF16, name="raw", tag="raw")
+            nc.sync.dma_start(out=raw[:], in_=row_tiles[order[i]])
+            raws[i] = raw
+            if i == 11:
                 nc.sync.dma_start(out=gain_bf[:], in_=q_gain.partition_broadcast(P))
 
         warm = const.tile([P, CHUNK], BF16, name="warm")
         nc.vector.memset(warm[:], 0.0)
+        idle_sum = accs.tile([P, CHUNK], F32, name="acc", tag="acc")
+
+        def keep_warm():
+            nc.tensor.matmul(out=idle_sum[:], lhsT=warm[:, 0:P], rhs=warm[:], start=True, stop=True)
+
+        for i in range(PRE_WARM):
+            keep_warm()
 
         t_int = const.tile([P, 4], I32, name="t_int")
         nc.gpsimd.iota(t_int[:], pattern=[[P, 4]], base=0, channel_multiplier=1)
@@ -150,65 +146,78 @@ def tile_causalselfattention_pa_kernel(tc, x, w_qkv_tern, q_gain, out_0, out_1, 
 
         state = {}
 
-        def keep_warm(bank):
-            nc.tensor.matmul(
-                out=bank[:].rearrange("p r u c -> p (r u c)"), lhsT=warm[:, 0:P], rhs=warm[:], start=True, stop=True
+        def sort_words(t):
+            sorted_words = sortp.tile([P, PASSES, 2, P], F32, name="sorted_words", tag="sorted_words")
+            nc.vector.tensor_copy(
+                out=sorted_words[:], in_=raws[t][:].bitcast(F32).rearrange("p (g i u) -> p g u i", g=PASSES, u=2)
             )
+            state["sorted", t] = sorted_words
 
         def transposes(t):
             banks = [tps.tile([P, 2, 2, P], F32, name="tp", tag="tp") for b in range(2)]
-            if t == 0:
-                for i in range(PRE_WARM):
-                    keep_warm(banks[0])
-            for r in range(4):
-                if t not in work and r % 2 == 0:
-                    keep_warm(banks[r // 2])
-                words = raws[t][:, r, :].bitcast(F32)
+            words = raws[t][:].bitcast(F32)
+            for g in range(PASSES):
                 for u in range(2):
-                    nc.tensor.transpose(banks[r // 2][:, r % 2, u, :], words[:, u : 2 * P : 2], ident[:])
+                    if 1 <= t <= SORTED_STEPS:
+                        src = state["sorted", t][:, g, u, :]
+                    else:
+                        src = words[:, 256 * g + u : 256 * (g + 1) : 2]
+                    nc.tensor.transpose(banks[g // 2][:, g % 2, u, :], src, ident[:])
+                if t < WARM_STEPS and g % 2 == 1:
+                    keep_warm()
             state["banks"] = banks
 
         def copies(t):
-            grp = grpp.tile([P, 16 * P], BF16, name="grp", tag="grp", align_bytes=64)
+            groups = []
             for b in range(2):
-                dst = grp[:, 8 * P * b : 8 * P * (b + 1)].bitcast(F32).rearrange("p (r c u) -> p r c u", r=2, u=2)
-                src = state["banks"][b][:].rearrange("p r u c -> p r c u")
+                grp = grpp.tile([P, 8 * P], BF16, name="grp", tag="grp", align_bytes=64)
+                dst = grp[:].bitcast(F32).rearrange("p (g c u) -> p g c u", g=2, u=2)
+                src = state["banks"][b][:].rearrange("p g u c -> p g c u")
                 if t < V_COPY_STEPS and b == 1:
                     nc.vector.tensor_copy(out=dst, in_=src)
                 else:
                     nc.scalar.copy(out=dst, in_=src)
-            state["grp", t] = grp
+                groups.append(grp)
+            state["groups", t] = groups
 
         def quantise(t):
-            b, g = order[t]
-            if b == 0:
-                codes, scales = x_codes, x_scales
+            tile_no = order[t]
+            if tile_no < X_TILES:
+                codes, scales, lo = x_codes, x_scales, P * tile_no
             else:
-                if g == 0:
-                    state["w_codes", b - 1] = codep.tile(
+                c = (tile_no - X_TILES) // 4
+                lo = P * ((tile_no - X_TILES) % 4)
+                if lo == 0:
+                    state["w_codes", c] = codep.tile(
                         [P, PASSES, CHUNK], U32, name="w_codes", tag="w_codes", align_bytes=64
                     )
-                    state["w_scales", b - 1] = codep.tile(
+                    state["w_scales", c] = codep.tile(
                         [P, PASSES, CHUNK], U8, name="w_scales", tag="w_scales", align_bytes=64
                     )
-                codes, scales = state["w_codes", b - 1], state["w_scales", b - 1]
-            nc.vector.quantize_mx(out=codes[:, g, :].bitcast(E5X4), scales=scales[:, g, :], in_=state["grp", t][:])
+                codes, scales = state["w_codes", c], state["w_scales", c]
+            for g in range(PASSES):
+                nc.vector.quantize_mx(
+                    out=codes[:, g, lo : lo + P].bitcast(E5X4),
+                    scales=scales[:, g, lo : lo + P],
+                    in_=state["groups", t][g // 2][:, 4 * P * (g % 2) : 4 * P * (g % 2 + 1)],
+                )
 
-        def matmul(c, m, g):
-            if g == 0:
+        def matmuls(c, m, passes):
+            if passes[0] == 0:
                 if c < ROPE_CHUNKS:
                     state["sum", c, m] = accs.tile([P, CHUNK], F32, name="acc", tag="acc")
                 else:
                     state["sum", c, m] = tps.tile([P, CHUNK], F32, name="tp", tag="tp")
-            nc.tensor.matmul_mx(
-                out=state["sum", c, m][:],
-                lhsT=x_codes[:, g, P * m : P * (m + 1)].bitcast(E5X4),
-                lhsT_scale=x_scales[:, g, P * m : P * (m + 1)],
-                rhs=state["w_codes", c][:, g, :].bitcast(E5X4),
-                rhs_scale=state["w_scales", c][:, g, :],
-                start=(g == 0),
-                stop=(g == PASSES - 1),
-            )
+            for g in passes:
+                nc.tensor.matmul_mx(
+                    out=state["sum", c, m][:],
+                    lhsT=x_codes[:, g, P * m : P * (m + 1)].bitcast(E5X4),
+                    lhsT_scale=x_scales[:, g, P * m : P * (m + 1)],
+                    rhs=state["w_codes", c][:, g, :].bitcast(E5X4),
+                    rhs_scale=state["w_scales", c][:, g, :],
+                    start=(g == 0),
+                    stop=(g == PASSES - 1),
+                )
 
         def squares(c, m):
             if m % 2 == 0:
@@ -229,65 +238,70 @@ def tile_causalselfattention_pa_kernel(tc, x, w_qkv_tern, q_gain, out_0, out_1, 
                 )
                 state["rstd", c, m // 2] = rstd
 
+        def factors(c, pair):
+            fac = epi.tile([P, 2, 4], F32, name="fac", tag="fac")
+            nc.vector.tensor_tensor(
+                out=fac[:],
+                in0=state["rstd", c, pair][:].rearrange("p (m h) -> p m h", m=2),
+                in1=gain[:, 4 * c : 4 * c + 4].unsqueeze(1).to_broadcast([P, 2, 4]),
+                op=ALU.mult,
+            )
+            state["fac", c, pair] = fac
+
         def rope(c, m):
-            pair = m // 2
-            if m % 2 == 0:
-                fac = epi.tile([P, 2, 4], F32, name="fac", tag="fac")
-                nc.vector.tensor_tensor(
-                    out=fac[:],
-                    in0=state["rstd", c, pair][:].rearrange("p (m h) -> p m h", m=2),
-                    in1=gain[:, 4 * c : 4 * c + 4].unsqueeze(1).to_broadcast([P, 2, 4]),
-                    op=ALU.mult,
-                )
-                state["fac"] = fac
-                state["prod"] = epi.tile([P, 8, 2, HEAD], F32, name="prod", tag="prod")
-            prod = state["prod"]
+            prod = epi.tile([P, 4, 2, HEAD], F32, name="prod", tag="prod")
             for h in range(4):
                 nc.vector.scalar_tensor_tensor(
-                    out=prod[:, 4 * (m % 2) + h, :, :],
+                    out=prod[:, h, :, :],
                     in0=state["sum", c, m][:, HEAD * h : HEAD * (h + 1)].unsqueeze(1).to_broadcast([P, 2, HEAD]),
-                    scalar=state["fac"][:, m % 2, h : h + 1],
+                    scalar=state["fac", c, m // 2][:, m % 2, h : h + 1],
                     in1=tab[:, m, :, :],
                     op0=ALU.mult,
                     op1=ALU.mult,
                 )
-            if m % 2 == 1:
-                res = outp.tile([P, 8, HEAD], F32, name="res", tag="res")
-                nc.vector.tensor_tensor(
-                    out=res[:, :, 0:HALF], in0=prod[:, :, 0, 0:HALF], in1=prod[:, :, 1, HALF:HEAD], op=ALU.add
-                )
-                nc.vector.tensor_tensor(
-                    out=res[:, :, HALF:HEAD], in0=prod[:, :, 0, HALF:HEAD], in1=prod[:, :, 1, 0:HALF], op=ALU.add
-                )
-                nc.sync.dma_start(
-                    out=dests[c].rearrange("(m p) n -> p m n", p=P)[:, 2 * pair : 2 * pair + 2, :],
-                    in_=res[:].rearrange("p (m h) d -> p m (h d)", m=2),
-                )
+            res = outp.tile([P, 4, HEAD], F32, name="res", tag="res")
+            nc.vector.tensor_tensor(
+                out=res[:, :, 0:HALF], in0=prod[:, :, 0, 0:HALF], in1=prod[:, :, 1, HALF:HEAD], op=ALU.add
+            )
+            nc.vector.tensor_tensor(
+                out=res[:, :, HALF:HEAD], in0=prod[:, :, 0, HALF:HEAD], in1=prod[:, :, 1, 0:HALF], op=ALU.add
+            )
+            nc.sync.dma_start(out=dests[c][P * m : P * (m + 1), :], in_=res[:].rearrange("p h d -> p (h d)"))
 
         def plain_out(c, m):
             res = outp.tile([P, CHUNK], F32, name="res", tag="res")
             nc.scalar.copy(out=res[:], in_=state["sum", c, m][:])
             nc.sync.dma_start(out=dests[c][P * m : P * (m + 1), :], in_=res[:])
 
-        waiting = []
-        for t in range(last_step + 4):
-            ready = len(waiting)
-            for c, m, g in work.get(t, []):
-                matmul(c, m, g)
-            if t < STEPS_T:
+        factor_at = {}
+        rope_at = {}
+        for t in range(WARM_STEPS + len(pieces) + 3):
+            q = t - WARM_STEPS
+            closed = None
+            if 0 <= q < len(pieces):
+                c, m, passes = pieces[q]
+                matmuls(c, m, passes)
+                if passes[-1] == PASSES - 1:
+                    closed = (c, m)
+            if t < ROW_TILES:
                 transposes(t)
-            for c, m, g in work.get(t, []):
-                if g == PASSES - 1:
-                    if c < ROPE_CHUNKS:
-                        squares(c, m)
-                        waiting.append((c, m))
-                    else:
-                        plain_out(c, m)
-            if ready > 0 and (ready > 1 or waiting[0][1] % 2 == 1):
-                c, m = waiting[0]
-                waiting.remove(waiting[0])
-                rope(c, m)
-            if 1 <= t <= STEPS_T:
+            if closed is not None:
+                c, m = closed
+                if c < ROPE_CHUNKS:
+                    squares(c, m)
+                    if m % 2 == 1:
+                        factor_at[t + 1] = (c, m // 2)
+                        rope_at[t + 1] = (c, m - 1)
+                        rope_at[t + 2] = (c, m)
+                else:
+                    plain_out(c, m)
+            if t < SORTED_STEPS:
+                sort_words(t + 1)
+            if 1 <= t <= ROW_TILES:
                 quantise(t - 1)
-            if t < STEPS_T:
+            if t in factor_at:
+                factors(factor_at[t][0], factor_at[t][1])
+            if t in rope_at:
+                rope(rope_at[t][0], rope_at[t][1])
+            if t < ROW_TILES:
                 copies(t)

@@ -16,27 +16,33 @@ P = 128
 K = 2048
 PASSES = 4
 TOKENS = 512
+TOKEN_TILES = 4
 HEAD = 128
 HALF = 64
 CHUNK = 512
-ROW_TILES = 28
-X_TILES = 4
+CHUNKS = 6
 ROPE_CHUNKS = 5
-PRE_WARM = 6
-WARM_STEPS = 7
-V_COPY_STEPS = 2
-SORTED_STEPS = 10
+X_TILES = 4
+ROW_TILES = 28
+Q_HEADS = 16
+
+LEAD_STEPS = 6
+FIRST_IDLE_MATMULS = 6
+VECTOR_COPY_STEPS = 2
+GAIN_LOAD_AFTER = 12
+
 RMS_EPS = 1.1920929e-07
 PI = 3.141592653589793
 PI_HI = 102944.0 / 32768.0
 PI_LO = PI - PI_HI
 FREQ_RATIO = 10000.0 ** (-1.0 / 64.0)
 
-FLOPS = 2 * TOKENS * K * 3072
+FLOPS = 2 * TOKENS * K * CHUNK * CHUNKS
 
 
 def tile_causalselfattention_pa_kernel(tc, x, w_qkv_tern, q_gain, out_0, out_1, out_2):
     nc = tc.nc
+
     x_rows = x.rearrange("b s k -> (b s) k")
     row_tiles = [x_rows[P * i : P * (i + 1), :] for i in range(X_TILES)]
     row_tiles.extend([w_qkv_tern[P * i : P * (i + 1), :] for i in range(ROW_TILES - X_TILES)])
@@ -47,261 +53,264 @@ def tile_causalselfattention_pa_kernel(tc, x, w_qkv_tern, q_gain, out_0, out_1, 
 
     order = [0, 4, 5, 6, 7, 1, 2, 3]
     order.extend(range(8, ROW_TILES))
-    pieces = []
-    for m in range(4):
-        pieces.append((0, m, (0, 1)))
-        pieces.append((0, m, (2, 3)))
-    for c in range(1, 6):
-        for m in range(4):
-            pieces.append((c, m, (0, 1, 2, 3)))
+    runs = []
+    for m in range(TOKEN_TILES):
+        runs.append((0, m, (0, 1)))
+        runs.append((0, m, (2, 3)))
+    for c in range(1, CHUNKS):
+        for m in range(TOKEN_TILES):
+            runs.append((c, m, (0, 1, 2, 3)))
 
     with ExitStack() as ctx:
         const = ctx.enter_context(tc.tile_pool(name="const", bufs=1))
-        rawp = ctx.enter_context(tc.tile_pool(name="rawp", bufs=ROW_TILES))
-        sortp = ctx.enter_context(tc.tile_pool(name="sortp", bufs=3))
-        grpp = ctx.enter_context(tc.tile_pool(name="grpp", bufs=6))
-        codep = ctx.enter_context(tc.tile_pool(name="codep", bufs=3))
-        epi = ctx.enter_context(tc.tile_pool(name="epi", bufs=3))
-        outp = ctx.enter_context(tc.tile_pool(name="outp", bufs=8))
-        tps = ctx.enter_context(tc.psum_pool(name="tps", bufs=4))
-        accs = ctx.enter_context(tc.psum_pool(name="accs", bufs=4))
+        raw_pool = ctx.enter_context(tc.tile_pool(name="raw_pool", bufs=ROW_TILES))
+        grouped_pool = ctx.enter_context(tc.tile_pool(name="grouped_pool", bufs=6))
+        code_pool = ctx.enter_context(tc.tile_pool(name="code_pool", bufs=3))
+        small_pool = ctx.enter_context(tc.tile_pool(name="small_pool", bufs=3))
+        out_pool = ctx.enter_context(tc.tile_pool(name="out_pool", bufs=5))
+        turn_pool = ctx.enter_context(tc.psum_pool(name="turn_pool", bufs=4))
+        sum_pool = ctx.enter_context(tc.psum_pool(name="sum_pool", bufs=4))
         ctx.enter_context(tc.manual_schedule())
 
-        gain_bf = const.tile([P, 16], BF16, name="gain_bf")
-        raws = {}
-        for i in range(ROW_TILES):
-            raw = rawp.tile([P, K], BF16, name="raw", tag="raw")
-            nc.sync.dma_start(out=raw[:], in_=row_tiles[order[i]])
-            raws[i] = raw
-            if i == 11:
+        gain_bf = const.tile([P, Q_HEADS], BF16, name="gain_bf")
+        raws = []
+        for step in range(ROW_TILES):
+            raw = raw_pool.tile([P, K], BF16, name="raw", tag="raw")
+            nc.sync.dma_start(out=raw[:], in_=row_tiles[order[step]])
+            raws.append(raw)
+            if step == GAIN_LOAD_AFTER - 1:
                 nc.sync.dma_start(out=gain_bf[:], in_=q_gain.partition_broadcast(P))
 
-        warm = const.tile([P, CHUNK], BF16, name="warm")
-        nc.vector.memset(warm[:], 0.0)
-        idle_sum = accs.tile([P, CHUNK], F32, name="acc", tag="acc")
+        zeros = const.tile([P, CHUNK], BF16, name="zeros")
+        nc.vector.memset(zeros[:], 0.0)
+        idle_sum = sum_pool.tile([P, CHUNK], F32, name="sums", tag="sums")
 
-        def keep_warm():
-            nc.tensor.matmul(out=idle_sum[:], lhsT=warm[:, 0:P], rhs=warm[:], start=True, stop=True)
+        def idle_matmul():
+            nc.tensor.matmul(out=idle_sum[:], lhsT=zeros[:, 0:P], rhs=zeros[:], start=True, stop=True)
 
-        for i in range(PRE_WARM):
-            keep_warm()
+        for i in range(FIRST_IDLE_MATMULS):
+            idle_matmul()
 
-        t_int = const.tile([P, 4], I32, name="t_int")
-        nc.gpsimd.iota(t_int[:], pattern=[[P, 4]], base=0, channel_multiplier=1)
+        token = const.tile([P, TOKEN_TILES], I32, name="token")
+        nc.gpsimd.iota(token[:], pattern=[[P, TOKEN_TILES]], base=0, channel_multiplier=1)
         ident = const.tile([P, P], F32, name="ident")
         make_identity(nc, ident[:])
-        gain = const.tile([P, 20], F32, name="gain")
+        gain = const.tile([P, Q_HEADS + 4], F32, name="gain")
         nc.gpsimd.memset(gain[:], 1.0)
 
-        half_ang = const.tile([P, 4, HALF], F32, name="half_ang")
+        half_angle = const.tile([P, TOKEN_TILES, HALF], F32, name="half_angle")
         nc.vector.tensor_scalar(
-            out=half_ang[:, :, 0:1], in0=t_int[:].unsqueeze(2), scalar1=0.5, scalar2=None, op0=ALU.mult
+            out=half_angle[:, :, 0:1], in0=token[:].unsqueeze(2), scalar1=0.5, scalar2=None, op0=ALU.mult
         )
         for width in (1, 4, 16):
-            for m in range(1, 4):
+            for i in range(1, 4):
                 nc.vector.tensor_scalar(
-                    out=half_ang[:, :, m * width : (m + 1) * width],
-                    in0=half_ang[:, :, 0:width],
-                    scalar1=FREQ_RATIO ** (m * width),
+                    out=half_angle[:, :, i * width : (i + 1) * width],
+                    in0=half_angle[:, :, 0:width],
+                    scalar1=FREQ_RATIO ** (i * width),
                     scalar2=None,
                     op0=ALU.mult,
                 )
-        turns = const.tile([P, 4, HALF], I32, name="turns")
+        turns = const.tile([P, TOKEN_TILES, HALF], I32, name="turns")
         nc.vector.tensor_scalar(
-            out=turns[:], in0=half_ang[:], scalar1=1.0 / PI, scalar2=0.1, op0=ALU.mult, op1=ALU.add
+            out=turns[:], in0=half_angle[:], scalar1=1.0 / PI, scalar2=0.1, op0=ALU.mult, op1=ALU.add
         )
-        red_hi = const.tile([P, 4, HALF], F32, name="red_hi")
+        reduced_hi = const.tile([P, TOKEN_TILES, HALF], F32, name="reduced_hi")
         nc.vector.scalar_tensor_tensor(
-            out=red_hi[:], in0=turns[:], scalar=-PI_HI, in1=half_ang[:], op0=ALU.mult, op1=ALU.add
+            out=reduced_hi[:], in0=turns[:], scalar=-PI_HI, in1=half_angle[:], op0=ALU.mult, op1=ALU.add
         )
-        red = const.tile([P, 4, HALF], F32, name="red")
+        reduced = const.tile([P, TOKEN_TILES, HALF], F32, name="reduced")
         nc.vector.scalar_tensor_tensor(
-            out=red[:], in0=turns[:], scalar=-PI_LO, in1=red_hi[:], op0=ALU.mult, op1=ALU.add
+            out=reduced[:], in0=turns[:], scalar=-PI_LO, in1=reduced_hi[:], op0=ALU.mult, op1=ALU.add
         )
-        sin_a = const.tile([P, 4, HALF], F32, name="sin_a")
-        nc.scalar.activation(out=sin_a[:], in_=red[:], func=ACT.Sin)
-        sin_b = const.tile([P, 4, HALF], F32, name="sin_b")
-        nc.scalar.activation(out=sin_b[:], in_=red[:], func=ACT.Sin, bias=-PI / 4.0)
-        first_rstd = const.tile([P, 1], F32, name="first_rstd")
-        nc.scalar.activation(out=first_rstd[:], in_=gain[:, 16:17], func=ACT.Abs_reciprocal_sqrt)
-        sq_a = const.tile([P, 4, HALF], F32, name="sq_a")
-        nc.gpsimd.tensor_tensor(out=sq_a[:], in0=sin_a[:], in1=sin_a[:], op=ALU.mult)
-        sq_b = const.tile([P, 4, HALF], F32, name="sq_b")
-        nc.gpsimd.tensor_tensor(out=sq_b[:], in0=sin_b[:], in1=sin_b[:], op=ALU.mult)
-        tab = const.tile([P, 4, 2, HEAD], F32, name="tab")
-        for row, lo, src, sign in ((0, 0, sq_a, 1.0), (0, HALF, sq_a, 1.0), (1, 0, sq_b, -1.0), (1, HALF, sq_b, 1.0)):
+        sin_for_cos = const.tile([P, TOKEN_TILES, HALF], F32, name="sin_for_cos")
+        nc.scalar.activation(out=sin_for_cos[:], in_=reduced[:], func=ACT.Sin)
+        sin_for_sin = const.tile([P, TOKEN_TILES, HALF], F32, name="sin_for_sin")
+        nc.scalar.activation(out=sin_for_sin[:], in_=reduced[:], func=ACT.Sin, bias=-PI / 4.0)
+        first_call = const.tile([P, 1], F32, name="first_call")
+        nc.scalar.activation(out=first_call[:], in_=gain[:, Q_HEADS : Q_HEADS + 1], func=ACT.Abs_reciprocal_sqrt)
+        square_for_cos = const.tile([P, TOKEN_TILES, HALF], F32, name="square_for_cos")
+        nc.gpsimd.tensor_tensor(out=square_for_cos[:], in0=sin_for_cos[:], in1=sin_for_cos[:], op=ALU.mult)
+        square_for_sin = const.tile([P, TOKEN_TILES, HALF], F32, name="square_for_sin")
+        nc.gpsimd.tensor_tensor(out=square_for_sin[:], in0=sin_for_sin[:], in1=sin_for_sin[:], op=ALU.mult)
+        table = const.tile([P, TOKEN_TILES, 2, HEAD], F32, name="table")
+        for row, first_col, square, sign in (
+            (0, 0, square_for_cos, 1.0),
+            (0, HALF, square_for_cos, 1.0),
+            (1, 0, square_for_sin, -1.0),
+            (1, HALF, square_for_sin, 1.0),
+        ):
             nc.gpsimd.tensor_scalar(
-                out=tab[:, :, row, lo : lo + HALF],
-                in0=src[:],
+                out=table[:, :, row, first_col : first_col + HALF],
+                in0=square[:],
                 scalar1=-2.0 * sign,
                 scalar2=sign,
                 op0=ALU.mult,
                 op1=ALU.add,
             )
-        nc.gpsimd.tensor_copy(out=gain[:, 0:16], in_=gain_bf[:])
+        nc.gpsimd.tensor_copy(out=gain[:, 0:Q_HEADS], in_=gain_bf[:])
 
-        junk = const.tile([P, HEAD], BF16, name="junk")
+        unread_squares = const.tile([P, HEAD], BF16, name="unread_squares")
         x_codes = const.tile([P, PASSES, TOKENS], U32, name="x_codes", align_bytes=64)
         x_scales = const.tile([P, PASSES, TOKENS], U8, name="x_scales", align_bytes=64)
+        w_codes = {}
+        w_scales = {}
 
-        state = {}
+        turned = {}
+        grouped = {}
+        sums = {}
+        square_sums = {}
+        rstd = {}
+        factor = {}
+        products = {}
 
-        def sort_words(t):
-            sorted_words = sortp.tile([P, PASSES, 2, P], F32, name="sorted_words", tag="sorted_words")
-            nc.vector.tensor_copy(
-                out=sorted_words[:], in_=raws[t][:].bitcast(F32).rearrange("p (g i u) -> p g u i", g=PASSES, u=2)
-            )
-            state["sorted", t] = sorted_words
-
-        def transposes(t):
-            banks = [tps.tile([P, 2, 2, P], F32, name="tp", tag="tp") for b in range(2)]
-            words = raws[t][:].bitcast(F32)
+        def transposes(step):
+            turned[step] = [turn_pool.tile([P, 2, 2, P], F32, name="turned", tag="turned") for b in range(2)]
+            words = raws[step][:].bitcast(F32)
             for g in range(PASSES):
                 for u in range(2):
-                    if 1 <= t <= SORTED_STEPS:
-                        src = state["sorted", t][:, g, u, :]
-                    else:
-                        src = words[:, 256 * g + u : 256 * (g + 1) : 2]
-                    nc.tensor.transpose(banks[g // 2][:, g % 2, u, :], src, ident[:])
-                if t < WARM_STEPS and g % 2 == 1:
-                    keep_warm()
-            state["banks"] = banks
+                    nc.tensor.transpose(
+                        turned[step][g // 2][:, g % 2, u, :], words[:, 256 * g + u : 256 * (g + 1) : 2], ident[:]
+                    )
+                if step < LEAD_STEPS and g % 2 == 1:
+                    idle_matmul()
 
-        def copies(t):
-            groups = []
+        def copies(step):
+            grouped[step] = []
             for b in range(2):
-                grp = grpp.tile([P, 8 * P], BF16, name="grp", tag="grp", align_bytes=64)
-                dst = grp[:].bitcast(F32).rearrange("p (g c u) -> p g c u", g=2, u=2)
-                src = state["banks"][b][:].rearrange("p g u c -> p g c u")
-                if t < V_COPY_STEPS and b == 1:
+                tile = grouped_pool.tile([P, 8 * P], BF16, name="grouped", tag="grouped", align_bytes=64)
+                dst = tile[:].bitcast(F32).rearrange("p (g c u) -> p g c u", g=2, u=2)
+                src = turned[step][b][:].rearrange("p g u c -> p g c u")
+                if step < VECTOR_COPY_STEPS and b == 1:
                     nc.vector.tensor_copy(out=dst, in_=src)
                 else:
                     nc.scalar.copy(out=dst, in_=src)
-                groups.append(grp)
-            state["groups", t] = groups
+                grouped[step].append(tile)
 
-        def quantise(t):
-            tile_no = order[t]
-            if tile_no < X_TILES:
-                codes, scales, lo = x_codes, x_scales, P * tile_no
+        def quantise(step):
+            row_tile = order[step]
+            if row_tile < X_TILES:
+                codes, scales, first_col = x_codes, x_scales, P * row_tile
             else:
-                c = (tile_no - X_TILES) // 4
-                lo = P * ((tile_no - X_TILES) % 4)
-                if lo == 0:
-                    state["w_codes", c] = codep.tile(
-                        [P, PASSES, CHUNK], U32, name="w_codes", tag="w_codes", align_bytes=64
-                    )
-                    state["w_scales", c] = codep.tile(
-                        [P, PASSES, CHUNK], U8, name="w_scales", tag="w_scales", align_bytes=64
-                    )
-                codes, scales = state["w_codes", c], state["w_scales", c]
+                c = (row_tile - X_TILES) // 4
+                first_col = P * ((row_tile - X_TILES) % 4)
+                if first_col == 0:
+                    w_codes[c] = code_pool.tile([P, PASSES, CHUNK], U32, name="w_codes", tag="w_codes", align_bytes=64)
+                    w_scales[c] = code_pool.tile([P, PASSES, CHUNK], U8, name="w_scales", tag="w_scales", align_bytes=64)
+                codes, scales = w_codes[c], w_scales[c]
             for g in range(PASSES):
                 nc.vector.quantize_mx(
-                    out=codes[:, g, lo : lo + P].bitcast(E5X4),
-                    scales=scales[:, g, lo : lo + P],
-                    in_=state["groups", t][g // 2][:, 4 * P * (g % 2) : 4 * P * (g % 2 + 1)],
+                    out=codes[:, g, first_col : first_col + P].bitcast(E5X4),
+                    scales=scales[:, g, first_col : first_col + P],
+                    in_=grouped[step][g // 2][:, 4 * P * (g % 2) : 4 * P * (g % 2 + 1)],
                 )
 
         def matmuls(c, m, passes):
             if passes[0] == 0:
                 if c < ROPE_CHUNKS:
-                    state["sum", c, m] = accs.tile([P, CHUNK], F32, name="acc", tag="acc")
+                    sums[c, m] = sum_pool.tile([P, CHUNK], F32, name="sums", tag="sums")
                 else:
-                    state["sum", c, m] = tps.tile([P, CHUNK], F32, name="tp", tag="tp")
+                    sums[c, m] = turn_pool.tile([P, CHUNK], F32, name="turned", tag="turned")
             for g in passes:
                 nc.tensor.matmul_mx(
-                    out=state["sum", c, m][:],
+                    out=sums[c, m][:],
                     lhsT=x_codes[:, g, P * m : P * (m + 1)].bitcast(E5X4),
                     lhsT_scale=x_scales[:, g, P * m : P * (m + 1)],
-                    rhs=state["w_codes", c][:, g, :].bitcast(E5X4),
-                    rhs_scale=state["w_scales", c][:, g, :],
+                    rhs=w_codes[c][:, g, :].bitcast(E5X4),
+                    rhs_scale=w_scales[c][:, g, :],
                     start=(g == 0),
                     stop=(g == PASSES - 1),
                 )
 
         def squares(c, m):
+            pair = m // 2
             if m % 2 == 0:
-                state["ssq", c] = epi.tile([P, 8], F32, name="ssq", tag="ssq")
-            ssq = state["ssq", c]
+                square_sums[c, pair] = small_pool.tile([P, 8], F32, name="square_sums", tag="square_sums")
             for h in range(4):
                 col = 4 * (m % 2) + h
                 nc.scalar.activation(
-                    out=junk[:],
-                    in_=state["sum", c, m][:, HEAD * h : HEAD * (h + 1)],
+                    out=unread_squares[:],
+                    in_=sums[c, m][:, HEAD * h : HEAD * (h + 1)],
                     func=ACT.Square,
-                    accum_out=ssq[:, col : col + 1],
+                    accum_out=square_sums[c, pair][:, col : col + 1],
                 )
             if m % 2 == 1:
-                rstd = epi.tile([P, 8], F32, name="rstd", tag="rstd")
+                rstd[c, pair] = small_pool.tile([P, 8], F32, name="rstd", tag="rstd")
                 nc.scalar.activation(
-                    out=rstd[:], in_=ssq[:], func=ACT.Abs_reciprocal_sqrt, scale=1.0 / HEAD, bias=RMS_EPS
+                    out=rstd[c, pair][:],
+                    in_=square_sums[c, pair][:],
+                    func=ACT.Abs_reciprocal_sqrt,
+                    scale=1.0 / HEAD,
+                    bias=RMS_EPS,
                 )
-                state["rstd", c, m // 2] = rstd
 
         def factors(c, pair):
-            fac = epi.tile([P, 2, 4], F32, name="fac", tag="fac")
+            factor[c, pair] = small_pool.tile([P, 2, 4], F32, name="factor", tag="factor")
             nc.vector.tensor_tensor(
-                out=fac[:],
-                in0=state["rstd", c, pair][:].rearrange("p (m h) -> p m h", m=2),
+                out=factor[c, pair][:],
+                in0=rstd[c, pair][:].rearrange("p (m h) -> p m h", m=2),
                 in1=gain[:, 4 * c : 4 * c + 4].unsqueeze(1).to_broadcast([P, 2, 4]),
                 op=ALU.mult,
             )
-            state["fac", c, pair] = fac
 
         def rope(c, m):
-            prod = epi.tile([P, 4, 2, HEAD], F32, name="prod", tag="prod")
+            pair = m // 2
+            if m % 2 == 0:
+                products[c, pair] = small_pool.tile([P, 8, 2, HEAD], F32, name="products", tag="products", bufs=2)
+            prod = products[c, pair]
             for h in range(4):
                 nc.vector.scalar_tensor_tensor(
-                    out=prod[:, h, :, :],
-                    in0=state["sum", c, m][:, HEAD * h : HEAD * (h + 1)].unsqueeze(1).to_broadcast([P, 2, HEAD]),
-                    scalar=state["fac", c, m // 2][:, m % 2, h : h + 1],
-                    in1=tab[:, m, :, :],
+                    out=prod[:, 4 * (m % 2) + h, :, :],
+                    in0=sums[c, m][:, HEAD * h : HEAD * (h + 1)].unsqueeze(1).to_broadcast([P, 2, HEAD]),
+                    scalar=factor[c, pair][:, m % 2, h : h + 1],
+                    in1=table[:, m, :, :],
                     op0=ALU.mult,
                     op1=ALU.mult,
                 )
-            res = outp.tile([P, 4, HEAD], F32, name="res", tag="res")
-            nc.vector.tensor_tensor(
-                out=res[:, :, 0:HALF], in0=prod[:, :, 0, 0:HALF], in1=prod[:, :, 1, HALF:HEAD], op=ALU.add
-            )
-            nc.vector.tensor_tensor(
-                out=res[:, :, HALF:HEAD], in0=prod[:, :, 0, HALF:HEAD], in1=prod[:, :, 1, 0:HALF], op=ALU.add
-            )
-            nc.sync.dma_start(out=dests[c][P * m : P * (m + 1), :], in_=res[:].rearrange("p h d -> p (h d)"))
+            if m % 2 == 1:
+                result = out_pool.tile([P, 8, HEAD], F32, name="result", tag="result")
+                nc.vector.tensor_tensor(
+                    out=result[:, :, 0:HALF], in0=prod[:, :, 0, 0:HALF], in1=prod[:, :, 1, HALF:HEAD], op=ALU.add
+                )
+                nc.vector.tensor_tensor(
+                    out=result[:, :, HALF:HEAD], in0=prod[:, :, 0, HALF:HEAD], in1=prod[:, :, 1, 0:HALF], op=ALU.add
+                )
+                nc.sync.dma_start(
+                    out=dests[c].rearrange("(m p) n -> p m n", p=P)[:, m - 1 : m + 1, :],
+                    in_=result[:].rearrange("p (m h) d -> p m (h d)", m=2),
+                )
 
         def plain_out(c, m):
-            res = outp.tile([P, CHUNK], F32, name="res", tag="res")
-            nc.scalar.copy(out=res[:], in_=state["sum", c, m][:])
-            nc.sync.dma_start(out=dests[c][P * m : P * (m + 1), :], in_=res[:])
+            result = out_pool.tile([P, CHUNK], F32, name="result", tag="result")
+            nc.scalar.copy(out=result[:], in_=sums[c, m][:])
+            nc.sync.dma_start(out=dests[c][P * m : P * (m + 1), :], in_=result[:])
 
-        factor_at = {}
-        rope_at = {}
-        for t in range(WARM_STEPS + len(pieces) + 3):
-            q = t - WARM_STEPS
+        factors_due = {}
+        rope_due = {}
+        for step in range(LEAD_STEPS + len(runs) + 3):
             closed = None
-            if 0 <= q < len(pieces):
-                c, m, passes = pieces[q]
+            if 0 <= step - LEAD_STEPS < len(runs):
+                c, m, passes = runs[step - LEAD_STEPS]
                 matmuls(c, m, passes)
                 if passes[-1] == PASSES - 1:
                     closed = (c, m)
-            if t < ROW_TILES:
-                transposes(t)
+            if step < ROW_TILES:
+                transposes(step)
             if closed is not None:
                 c, m = closed
                 if c < ROPE_CHUNKS:
                     squares(c, m)
                     if m % 2 == 1:
-                        factor_at[t + 1] = (c, m // 2)
-                        rope_at[t + 1] = (c, m - 1)
-                        rope_at[t + 2] = (c, m)
+                        factors_due[step + 1] = (c, m // 2)
+                        rope_due[step + 1] = (c, m - 1)
+                        rope_due[step + 2] = (c, m)
                 else:
                     plain_out(c, m)
-            if t < SORTED_STEPS:
-                sort_words(t + 1)
-            if 1 <= t <= ROW_TILES:
-                quantise(t - 1)
-            if t in factor_at:
-                factors(factor_at[t][0], factor_at[t][1])
-            if t in rope_at:
-                rope(rope_at[t][0], rope_at[t][1])
-            if t < ROW_TILES:
-                copies(t)
+            if step in factors_due:
+                factors(factors_due[step][0], factors_due[step][1])
+            if step in rope_due:
+                rope(rope_due[step][0], rope_due[step][1])
+            if 1 <= step <= ROW_TILES:
+                quantise(step - 1)
+            if step < ROW_TILES:
+                copies(step)

@@ -172,8 +172,9 @@ def tile_causalselfattention_pa_kernel(tc, x, w_qkv_tern, q_gain, out_0, out_1, 
                     nc.tensor.transpose(
                         turned[step][g // 2][:, g % 2, u, :], words[:, 256 * g + u : 256 * (g + 1) : 2], ident[:]
                     )
-                if step < LEAD_STEPS and g % 2 == 1:
-                    idle_matmul()
+            if step < LEAD_STEPS:
+                idle_matmul()
+                idle_matmul()
 
         def copies(step):
             grouped[step] = []

@@ -28,8 +28,14 @@ Q_HEADS = 16
 
 LEAD_STEPS = 6
 FIRST_IDLE_MATMULS = 6
-VECTOR_COPY_STEPS = 2
+VECTOR_COPY_STEPS = (0, 1) + tuple(range(15, 28, 2))
 GAIN_LOAD_AFTER = 12
+ADDS_AFTER_QUANT = True
+MERGED_ADD = False
+EARLY = 0
+Q_BEFORE_FIRST_PRODUCTS = True
+TURN_BUFS = 4
+SUM_BUFS = 4
 
 RMS_EPS = 1.1920929e-07
 PI = 3.141592653589793
@@ -55,8 +61,13 @@ def tile_causalselfattention_pa_kernel(tc, x, w_qkv_tern, q_gain, out_0, out_1, 
     order.extend(range(8, ROW_TILES))
     runs = []
     for m in range(TOKEN_TILES):
-        runs.append((0, m, (0, 1)))
-        runs.append((0, m, (2, 3)))
+        if m < EARLY:
+            runs.append((0, m, (0, 1, 2, 3)))
+        else:
+            runs.append((0, m, (0, 1)))
+            runs.append((0, m, (2, 3)))
+    for m in range(EARLY):
+        runs.append(None)
     for c in range(1, CHUNKS):
         for m in range(TOKEN_TILES):
             runs.append((c, m, (0, 1, 2, 3)))
@@ -68,8 +79,8 @@ def tile_causalselfattention_pa_kernel(tc, x, w_qkv_tern, q_gain, out_0, out_1, 
         code_pool = ctx.enter_context(tc.tile_pool(name="code_pool", bufs=3))
         small_pool = ctx.enter_context(tc.tile_pool(name="small_pool", bufs=3))
         out_pool = ctx.enter_context(tc.tile_pool(name="out_pool", bufs=5))
-        turn_pool = ctx.enter_context(tc.psum_pool(name="turn_pool", bufs=4))
-        sum_pool = ctx.enter_context(tc.psum_pool(name="sum_pool", bufs=4))
+        turn_pool = ctx.enter_context(tc.psum_pool(name="turn_pool", bufs=TURN_BUFS))
+        sum_pool = ctx.enter_context(tc.psum_pool(name="sum_pool", bufs=SUM_BUFS))
         ctx.enter_context(tc.manual_schedule())
 
         gain_bf = const.tile([P, Q_HEADS], BF16, name="gain_bf")
@@ -150,7 +161,7 @@ def tile_causalselfattention_pa_kernel(tc, x, w_qkv_tern, q_gain, out_0, out_1, 
             )
         nc.gpsimd.tensor_copy(out=gain[:, 0:Q_HEADS], in_=gain_bf[:])
 
-        unread_squares = const.tile([P, HEAD], BF16, name="unread_squares")
+        unread_squares = const.tile([P, 8, HEAD], BF16, name="unread_squares")
         x_codes = const.tile([P, PASSES, TOKENS], U32, name="x_codes", align_bytes=64)
         x_scales = const.tile([P, PASSES, TOKENS], U8, name="x_scales", align_bytes=64)
         w_codes = {}
@@ -168,6 +179,14 @@ def tile_causalselfattention_pa_kernel(tc, x, w_qkv_tern, q_gain, out_0, out_1, 
             turned[step] = [turn_pool.tile([P, 2, 2, P], F32, name="turned", tag="turned") for b in range(2)]
             words = raws[step][:].bitcast(F32)
             for g in range(PASSES):
+                if step >= LEAD_STEPS and runs[step - LEAD_STEPS] is None and g % 2 == 0:
+                    nc.tensor.matmul(
+                        out=turned[step][g // 2][:].rearrange("p g u c -> p (g u c)"),
+                        lhsT=zeros[:, 0:P],
+                        rhs=zeros[:],
+                        start=True,
+                        stop=True,
+                    )
                 for u in range(2):
                     nc.tensor.transpose(
                         turned[step][g // 2][:, g % 2, u, :], words[:, 256 * g + u : 256 * (g + 1) : 2], ident[:]
@@ -182,7 +201,7 @@ def tile_causalselfattention_pa_kernel(tc, x, w_qkv_tern, q_gain, out_0, out_1, 
                 tile = grouped_pool.tile([P, 8 * P], BF16, name="grouped", tag="grouped", align_bytes=64)
                 dst = tile[:].bitcast(F32).rearrange("p (g c u) -> p g c u", g=2, u=2)
                 src = turned[step][b][:].rearrange("p g u c -> p g c u")
-                if step < VECTOR_COPY_STEPS and b == 1:
+                if step in VECTOR_COPY_STEPS and b == 1:
                     nc.vector.tensor_copy(out=dst, in_=src)
                 else:
                     nc.scalar.copy(out=dst, in_=src)
@@ -230,7 +249,7 @@ def tile_causalselfattention_pa_kernel(tc, x, w_qkv_tern, q_gain, out_0, out_1, 
             for h in range(4):
                 col = 4 * (m % 2) + h
                 nc.scalar.activation(
-                    out=unread_squares[:],
+                    out=unread_squares[:, col, :],
                     in_=sums[c, m][:, HEAD * h : HEAD * (h + 1)],
                     func=ACT.Square,
                     accum_out=square_sums[c, pair][:, col : col + 1],
@@ -268,14 +287,27 @@ def tile_causalselfattention_pa_kernel(tc, x, w_qkv_tern, q_gain, out_0, out_1, 
                     op0=ALU.mult,
                     op1=ALU.mult,
                 )
-            if m % 2 == 1:
+            if m % 2 == 1 and not ADDS_AFTER_QUANT:
+                adds(c, m)
+
+        def adds(c, m):
+            prod = products[c, m // 2]
+            if True:
                 result = out_pool.tile([P, 8, HEAD], F32, name="result", tag="result")
-                nc.vector.tensor_tensor(
-                    out=result[:, :, 0:HALF], in0=prod[:, :, 0, 0:HALF], in1=prod[:, :, 1, HALF:HEAD], op=ALU.add
-                )
-                nc.vector.tensor_tensor(
-                    out=result[:, :, HALF:HEAD], in0=prod[:, :, 0, HALF:HEAD], in1=prod[:, :, 1, 0:HALF], op=ALU.add
-                )
+                if MERGED_ADD:
+                    nc.vector.tensor_tensor(
+                        out=result[:].rearrange("p h (f j) -> p h f j", f=2),
+                        in0=prod[:, :, 0, :].rearrange("p h (f j) -> p h f j", f=2),
+                        in1=prod[:, :, 1, :].rearrange("p h (f j) -> p h f j", f=2)[:, :, ::-1, :],
+                        op=ALU.add,
+                    )
+                else:
+                    nc.vector.tensor_tensor(
+                        out=result[:, :, 0:HALF], in0=prod[:, :, 0, 0:HALF], in1=prod[:, :, 1, HALF:HEAD], op=ALU.add
+                    )
+                    nc.vector.tensor_tensor(
+                        out=result[:, :, HALF:HEAD], in0=prod[:, :, 0, HALF:HEAD], in1=prod[:, :, 1, 0:HALF], op=ALU.add
+                    )
                 nc.sync.dma_start(
                     out=dests[c].rearrange("(m p) n -> p m n", p=P)[:, m - 1 : m + 1, :],
                     in_=result[:].rearrange("p (m h) d -> p m (h d)", m=2),
@@ -290,7 +322,7 @@ def tile_causalselfattention_pa_kernel(tc, x, w_qkv_tern, q_gain, out_0, out_1, 
         rope_due = {}
         for step in range(LEAD_STEPS + len(runs) + 3):
             closed = None
-            if 0 <= step - LEAD_STEPS < len(runs):
+            if 0 <= step - LEAD_STEPS < len(runs) and runs[step - LEAD_STEPS] is not None:
                 c, m, passes = runs[step - LEAD_STEPS]
                 matmuls(c, m, passes)
                 if passes[-1] == PASSES - 1:
@@ -309,9 +341,16 @@ def tile_causalselfattention_pa_kernel(tc, x, w_qkv_tern, q_gain, out_0, out_1, 
                     plain_out(c, m)
             if step in factors_due:
                 factors(factors_due[step][0], factors_due[step][1])
-            if step in rope_due:
+            if Q_BEFORE_FIRST_PRODUCTS and step in factors_due:
+                if 1 <= step <= ROW_TILES:
+                    quantise(step - 1)
                 rope(rope_due[step][0], rope_due[step][1])
-            if 1 <= step <= ROW_TILES:
-                quantise(step - 1)
+            else:
+                if step in rope_due:
+                    rope(rope_due[step][0], rope_due[step][1])
+                if 1 <= step <= ROW_TILES:
+                    quantise(step - 1)
+            if ADDS_AFTER_QUANT and step in rope_due and rope_due[step][1] % 2 == 1:
+                adds(rope_due[step][0], rope_due[step][1])
             if step < ROW_TILES:
                 copies(step)

@@ -27,8 +27,11 @@ ROW_TILES = 28
 Q_HEADS = 16
 
 LEAD_STEPS = 6
-FIRST_IDLE_MATMULS = 6
-VECTOR_COPY_STEPS = (0, 1) + tuple(range(15, 28, 2))
+FIRST_IDLE_MATMULS = 3
+SPLIT_FIRST = True
+IDLE_STEPS = 5
+LAST_BY_BANK = True
+VECTOR_COPY_STEPS = (0, 1) + tuple(range(14, 25, 2))
 GAIN_LOAD_AFTER = 12
 ADDS_AFTER_QUANT = True
 MERGED_ADD = False
@@ -79,13 +82,24 @@ def tile_causalselfattention_pa_kernel(tc, x, w_qkv_tern, q_gain, out_0, out_1, 
         code_pool = ctx.enter_context(tc.tile_pool(name="code_pool", bufs=3))
         small_pool = ctx.enter_context(tc.tile_pool(name="small_pool", bufs=3))
         out_pool = ctx.enter_context(tc.tile_pool(name="out_pool", bufs=5))
+        plain_pool = ctx.enter_context(tc.tile_pool(name="plain_pool", bufs=TOKEN_TILES))
         turn_pool = ctx.enter_context(tc.psum_pool(name="turn_pool", bufs=TURN_BUFS))
         sum_pool = ctx.enter_context(tc.psum_pool(name="sum_pool", bufs=SUM_BUFS))
         ctx.enter_context(tc.manual_schedule())
 
         gain_bf = const.tile([P, Q_HEADS], BF16, name="gain_bf")
         raws = []
+        first_raws = []
         for step in range(ROW_TILES):
+            if step == 0 and SPLIT_FIRST:
+                for g in range(PASSES):
+                    piece = const.tile([P, K // PASSES], BF16, name="first_raw%d" % g)
+                    nc.sync.dma_start(
+                        out=piece[:], in_=row_tiles[order[0]][:, (K // PASSES) * g : (K // PASSES) * (g + 1)]
+                    )
+                    first_raws.append(piece)
+                raws.append(None)
+                continue
             raw = raw_pool.tile([P, K], BF16, name="raw", tag="raw")
             nc.sync.dma_start(out=raw[:], in_=row_tiles[order[step]])
             raws.append(raw)
@@ -177,7 +191,6 @@ def tile_causalselfattention_pa_kernel(tc, x, w_qkv_tern, q_gain, out_0, out_1, 
 
         def transposes(step):
             turned[step] = [turn_pool.tile([P, 2, 2, P], F32, name="turned", tag="turned") for b in range(2)]
-            words = raws[step][:].bitcast(F32)
             for g in range(PASSES):
                 if step >= LEAD_STEPS and runs[step - LEAD_STEPS] is None and g % 2 == 0:
                     nc.tensor.matmul(
@@ -188,10 +201,12 @@ def tile_causalselfattention_pa_kernel(tc, x, w_qkv_tern, q_gain, out_0, out_1, 
                         stop=True,
                     )
                 for u in range(2):
-                    nc.tensor.transpose(
-                        turned[step][g // 2][:, g % 2, u, :], words[:, 256 * g + u : 256 * (g + 1) : 2], ident[:]
-                    )
-            if step < LEAD_STEPS:
+                    if step == 0 and SPLIT_FIRST:
+                        words = first_raws[g][:].bitcast(F32)[:, u:256:2]
+                    else:
+                        words = raws[step][:].bitcast(F32)[:, 256 * g + u : 256 * (g + 1) : 2]
+                    nc.tensor.transpose(turned[step][g // 2][:, g % 2, u, :], words, ident[:])
+            if step < IDLE_STEPS:
                 idle_matmul()
                 idle_matmul()
 
@@ -292,7 +307,20 @@ def tile_causalselfattention_pa_kernel(tc, x, w_qkv_tern, q_gain, out_0, out_1, 
 
         def adds(c, m):
             prod = products[c, m // 2]
-            if True:
+            if LAST_BY_BANK and c == ROPE_CHUNKS - 1 and m == TOKEN_TILES - 1:
+                for mm in (m - 1, m):
+                    rows = slice(4 * (mm % 2), 4 * (mm % 2) + 4)
+                    result = out_pool.tile([P, 4, HEAD], F32, name="result", tag="result")
+                    nc.vector.tensor_tensor(
+                        out=result[:, :, 0:HALF], in0=prod[:, rows, 0, 0:HALF], in1=prod[:, rows, 1, HALF:HEAD], op=ALU.add
+                    )
+                    nc.vector.tensor_tensor(
+                        out=result[:, :, HALF:HEAD], in0=prod[:, rows, 0, HALF:HEAD], in1=prod[:, rows, 1, 0:HALF], op=ALU.add
+                    )
+                    nc.sync.dma_start(
+                        out=dests[c][P * mm : P * (mm + 1), :], in_=result[:].rearrange("p h d -> p (h d)")
+                    )
+            else:
                 result = out_pool.tile([P, 8, HEAD], F32, name="result", tag="result")
                 if MERGED_ADD:
                     nc.vector.tensor_tensor(
@@ -314,9 +342,9 @@ def tile_causalselfattention_pa_kernel(tc, x, w_qkv_tern, q_gain, out_0, out_1, 
                 )
 
         def plain_out(c, m):
-            result = out_pool.tile([P, CHUNK], F32, name="result", tag="result")
-            nc.scalar.copy(out=result[:], in_=sums[c, m][:])
-            nc.sync.dma_start(out=dests[c][P * m : P * (m + 1), :], in_=result[:])
+            plain = plain_pool.tile([P, CHUNK], F32, name="plain", tag="plain")
+            nc.scalar.copy(out=plain[:], in_=sums[c, m][:])
+            nc.scalar.dma_start(out=dests[c][P * m : P * (m + 1), :], in_=plain[:])
 
         factors_due = {}
         rope_due = {}

@@ -29,6 +29,8 @@ Q_HEADS = 16
 LEAD_STEPS = 6
 FIRST_IDLE_MATMULS = 3
 SPLIT_FIRST = True
+VECTOR_SORTS = tuple(range(6, 12))
+SORT_AHEAD = 2
 IDLE_STEPS = 5
 LAST_BY_BANK = True
 VECTOR_COPY_STEPS = (0, 1) + tuple(range(14, 25, 2))
@@ -77,7 +79,8 @@ def tile_causalselfattention_pa_kernel(tc, x, w_qkv_tern, q_gain, out_0, out_1, 
 
     with ExitStack() as ctx:
         const = ctx.enter_context(tc.tile_pool(name="const", bufs=1))
-        raw_pool = ctx.enter_context(tc.tile_pool(name="raw_pool", bufs=ROW_TILES))
+        raw_pool = ctx.enter_context(tc.tile_pool(name="raw_pool", bufs=ROW_TILES - 1))
+        sorted_pool = ctx.enter_context(tc.tile_pool(name="sorted_pool", bufs=SORT_AHEAD + 1))
         grouped_pool = ctx.enter_context(tc.tile_pool(name="grouped_pool", bufs=6))
         code_pool = ctx.enter_context(tc.tile_pool(name="code_pool", bufs=3))
         small_pool = ctx.enter_context(tc.tile_pool(name="small_pool", bufs=3))
@@ -181,6 +184,7 @@ def tile_causalselfattention_pa_kernel(tc, x, w_qkv_tern, q_gain, out_0, out_1, 
         w_codes = {}
         w_scales = {}
 
+        sorted_rows = {}
         turned = {}
         grouped = {}
         sums = {}
@@ -188,6 +192,13 @@ def tile_causalselfattention_pa_kernel(tc, x, w_qkv_tern, q_gain, out_0, out_1, 
         rstd = {}
         factor = {}
         products = {}
+
+        def sort_words(step):
+            sorted_rows[step] = sorted_pool.tile([P, K], BF16, name="sorted_rows", tag="sorted_rows")
+            nc.vector.tensor_copy(
+                out=sorted_rows[step][:].bitcast(F32).rearrange("p (g u j) -> p g u j", g=PASSES, u=2),
+                in_=raws[step][:].bitcast(F32).rearrange("p (g j u) -> p g u j", g=PASSES, u=2),
+            )
 
         def transposes(step):
             turned[step] = [turn_pool.tile([P, 2, 2, P], F32, name="turned", tag="turned") for b in range(2)]
@@ -201,7 +212,9 @@ def tile_causalselfattention_pa_kernel(tc, x, w_qkv_tern, q_gain, out_0, out_1, 
                         stop=True,
                     )
                 for u in range(2):
-                    if step == 0 and SPLIT_FIRST:
+                    if step in sorted_rows:
+                        words = sorted_rows[step][:].bitcast(F32)[:, 256 * g + P * u : 256 * g + P * (u + 1)]
+                    elif step == 0 and SPLIT_FIRST:
                         words = first_raws[g][:].bitcast(F32)[:, u:256:2]
                     else:
                         words = raws[step][:].bitcast(F32)[:, 256 * g + u : 256 * (g + 1) : 2]
@@ -380,5 +393,7 @@ def tile_causalselfattention_pa_kernel(tc, x, w_qkv_tern, q_gain, out_0, out_1, 
                     quantise(step - 1)
             if ADDS_AFTER_QUANT and step in rope_due and rope_due[step][1] % 2 == 1:
                 adds(rope_due[step][0], rope_due[step][1])
+            if step + SORT_AHEAD in VECTOR_SORTS:
+                sort_words(step + SORT_AHEAD)
             if step < ROW_TILES:
                 copies(step)

@@ -201,11 +201,11 @@ def tile_causalselfattention_pa_kernel(tc, x, w_qkv_tern, q_gain, out_0, out_1, 
             )
 
         def transposes(step):
-            turned[step] = [turn_pool.tile([P, 2, 2, P], F32, name="turned", tag="turned") for b in range(2)]
+            turned[step] = [turn_pool.tile([P, 2, 2 * P], F32, name="turned", tag="turned") for b in range(2)]
             for g in range(PASSES):
                 if step >= LEAD_STEPS and runs[step - LEAD_STEPS] is None and g % 2 == 0:
                     nc.tensor.matmul(
-                        out=turned[step][g // 2][:].rearrange("p g u c -> p (g u c)"),
+                        out=turned[step][g // 2][:].rearrange("p u c -> p (u c)"),
                         lhsT=zeros[:, 0:P],
                         rhs=zeros[:],
                         start=True,
@@ -218,7 +218,7 @@ def tile_causalselfattention_pa_kernel(tc, x, w_qkv_tern, q_gain, out_0, out_1, 
                         words = first_raws[g][:].bitcast(F32)[:, u:256:2]
                     else:
                         words = raws[step][:].bitcast(F32)[:, 256 * g + u : 256 * (g + 1) : 2]
-                    nc.tensor.transpose(turned[step][g // 2][:, g % 2, u, :], words, ident[:])
+                    nc.tensor.transpose(turned[step][g // 2][:, u, P * (g % 2) : P * (g % 2 + 1)], words, ident[:])
             if step < IDLE_STEPS:
                 idle_matmul()
                 idle_matmul()
@@ -227,8 +227,8 @@ def tile_causalselfattention_pa_kernel(tc, x, w_qkv_tern, q_gain, out_0, out_1, 
             grouped[step] = []
             for b in range(2):
                 tile = grouped_pool.tile([P, 8 * P], BF16, name="grouped", tag="grouped", align_bytes=64)
-                dst = tile[:].bitcast(F32).rearrange("p (g c u) -> p g c u", g=2, u=2)
-                src = turned[step][b][:].rearrange("p g u c -> p g c u")
+                dst = tile[:].bitcast(F32).rearrange("p (c i u) -> p c u i", i=2, u=2)
+                src = turned[step][b][:].rearrange("p u (c i) -> p c u i", i=2)
                 if step in VECTOR_COPY_STEPS and b == 1:
                     nc.vector.tensor_copy(out=dst, in_=src)
                 else:

@@ -31,9 +31,12 @@ FIRST_IDLE_MATMULS = 3
 SPLIT_FIRST = True
 VECTOR_SORTS = tuple(range(6, 12))
 SORT_AHEAD = 2
+LOADS_AHEAD = 20
 IDLE_STEPS = 5
 LAST_BY_BANK = True
-VECTOR_COPY_STEPS = (0, 1) + tuple(range(14, 25, 2))
+VECTOR_COPIES = [(0, 1), (1, 1), (5, 0), (5, 1)] + [(s, 1) for s in range(14, 25, 2)]
+SINES_AFTER_STEP = 1
+NORM_TABLE_AFTER_STEP = 4
 GAIN_LOAD_AFTER = 12
 ADDS_AFTER_QUANT = True
 MERGED_ADD = False
@@ -79,11 +82,11 @@ def tile_causalselfattention_pa_kernel(tc, x, w_qkv_tern, q_gain, out_0, out_1, 
 
     with ExitStack() as ctx:
         const = ctx.enter_context(tc.tile_pool(name="const", bufs=1))
-        raw_pool = ctx.enter_context(tc.tile_pool(name="raw_pool", bufs=ROW_TILES - 1))
+        raw_pool = ctx.enter_context(tc.tile_pool(name="raw_pool", bufs=LOADS_AHEAD))
         sorted_pool = ctx.enter_context(tc.tile_pool(name="sorted_pool", bufs=SORT_AHEAD + 1))
-        grouped_pool = ctx.enter_context(tc.tile_pool(name="grouped_pool", bufs=6))
+        grouped_pool = ctx.enter_context(tc.tile_pool(name="grouped_pool", bufs=14))
         code_pool = ctx.enter_context(tc.tile_pool(name="code_pool", bufs=3))
-        small_pool = ctx.enter_context(tc.tile_pool(name="small_pool", bufs=3))
+        small_pool = ctx.enter_context(tc.tile_pool(name="small_pool", bufs=2 * ROPE_CHUNKS))
         out_pool = ctx.enter_context(tc.tile_pool(name="out_pool", bufs=5))
         plain_pool = ctx.enter_context(tc.tile_pool(name="plain_pool", bufs=TOKEN_TILES))
         turn_pool = ctx.enter_context(tc.psum_pool(name="turn_pool", bufs=TURN_BUFS))
@@ -93,7 +96,13 @@ def tile_causalselfattention_pa_kernel(tc, x, w_qkv_tern, q_gain, out_0, out_1, 
         gain_bf = const.tile([P, Q_HEADS], BF16, name="gain_bf")
         raws = []
         first_raws = []
-        for step in range(ROW_TILES):
+
+        def load(step):
+            raw = raw_pool.tile([P, K], BF16, name="raw", tag="raw")
+            nc.sync.dma_start(out=raw[:], in_=row_tiles[order[step]])
+            raws.append(raw)
+
+        for step in range(LOADS_AHEAD + 1):
             if step == 0 and SPLIT_FIRST:
                 for g in range(PASSES):
                     piece = const.tile([P, K // PASSES], BF16, name="first_raw%d" % g)
@@ -103,9 +112,7 @@ def tile_causalselfattention_pa_kernel(tc, x, w_qkv_tern, q_gain, out_0, out_1, 
                     first_raws.append(piece)
                 raws.append(None)
                 continue
-            raw = raw_pool.tile([P, K], BF16, name="raw", tag="raw")
-            nc.sync.dma_start(out=raw[:], in_=row_tiles[order[step]])
-            raws.append(raw)
+            load(step)
             if step == GAIN_LOAD_AFTER - 1:
                 nc.sync.dma_start(out=gain_bf[:], in_=q_gain.partition_broadcast(P))
 
@@ -152,33 +159,44 @@ def tile_causalselfattention_pa_kernel(tc, x, w_qkv_tern, q_gain, out_0, out_1, 
             out=reduced[:], in0=turns[:], scalar=-PI_LO, in1=reduced_hi[:], op0=ALU.mult, op1=ALU.add
         )
         sin_for_cos = const.tile([P, TOKEN_TILES, HALF], F32, name="sin_for_cos")
-        nc.scalar.activation(out=sin_for_cos[:], in_=reduced[:], func=ACT.Sin)
         sin_for_sin = const.tile([P, TOKEN_TILES, HALF], F32, name="sin_for_sin")
-        nc.scalar.activation(out=sin_for_sin[:], in_=reduced[:], func=ACT.Sin, bias=-PI / 4.0)
-        first_call = const.tile([P, 1], F32, name="first_call")
-        nc.scalar.activation(out=first_call[:], in_=gain[:, Q_HEADS : Q_HEADS + 1], func=ACT.Abs_reciprocal_sqrt)
-        square_for_cos = const.tile([P, TOKEN_TILES, HALF], F32, name="square_for_cos")
-        nc.gpsimd.tensor_tensor(out=square_for_cos[:], in0=sin_for_cos[:], in1=sin_for_cos[:], op=ALU.mult)
-        square_for_sin = const.tile([P, TOKEN_TILES, HALF], F32, name="square_for_sin")
-        nc.gpsimd.tensor_tensor(out=square_for_sin[:], in0=sin_for_sin[:], in1=sin_for_sin[:], op=ALU.mult)
-        table = const.tile([P, TOKEN_TILES, 2, HEAD], F32, name="table")
-        for row, first_col, square, sign in (
-            (0, 0, square_for_cos, 1.0),
-            (0, HALF, square_for_cos, 1.0),
-            (1, 0, square_for_sin, -1.0),
-            (1, HALF, square_for_sin, 1.0),
-        ):
-            nc.gpsimd.tensor_scalar(
-                out=table[:, :, row, first_col : first_col + HALF],
-                in0=square[:],
-                scalar1=-2.0 * sign,
-                scalar2=sign,
-                op0=ALU.mult,
-                op1=ALU.add,
-            )
-        nc.gpsimd.tensor_copy(out=gain[:, 0:Q_HEADS], in_=gain_bf[:])
+        first_call = const.tile([P, 2], F32, name="first_call")
+        nc.scalar.activation(out=first_call[:, 0:1], in_=gain[:, Q_HEADS : Q_HEADS + 1], func=ACT.Sin)
 
-        unread_squares = const.tile([P, 8, HEAD], BF16, name="unread_squares")
+        def sines():
+            nc.scalar.activation(out=sin_for_cos[:], in_=reduced[:], func=ACT.Sin)
+            nc.scalar.activation(out=sin_for_sin[:], in_=reduced[:], func=ACT.Sin, bias=-PI / 4.0)
+
+        def norm_table():
+            nc.scalar.activation(
+                out=first_call[:, 1:2], in_=gain[:, Q_HEADS : Q_HEADS + 1], func=ACT.Abs_reciprocal_sqrt
+            )
+
+        square_for_cos = const.tile([P, TOKEN_TILES, HALF], F32, name="square_for_cos")
+        square_for_sin = const.tile([P, TOKEN_TILES, HALF], F32, name="square_for_sin")
+        table = const.tile([P, TOKEN_TILES, 2, HEAD], F32, name="table")
+
+        def tables():
+            nc.gpsimd.tensor_tensor(out=square_for_cos[:], in0=sin_for_cos[:], in1=sin_for_cos[:], op=ALU.mult)
+            nc.gpsimd.tensor_tensor(out=square_for_sin[:], in0=sin_for_sin[:], in1=sin_for_sin[:], op=ALU.mult)
+            for row, first_col, square, sign in (
+                (0, 0, square_for_cos, 1.0),
+                (0, HALF, square_for_cos, 1.0),
+                (1, 0, square_for_sin, -1.0),
+                (1, HALF, square_for_sin, 1.0),
+            ):
+                nc.gpsimd.tensor_scalar(
+                    out=table[:, :, row, first_col : first_col + HALF],
+                    in0=square[:],
+                    scalar1=-2.0 * sign,
+                    scalar2=sign,
+                    op0=ALU.mult,
+                    op1=ALU.add,
+                )
+            nc.gpsimd.tensor_copy(out=gain[:, 0:Q_HEADS], in_=gain_bf[:])
+
+
+        unread_squares = const.tile([P, 20, HEAD], BF16, name="unread_squares")
         x_codes = const.tile([P, PASSES, TOKENS], U32, name="x_codes", align_bytes=64)
         x_scales = const.tile([P, PASSES, TOKENS], U8, name="x_scales", align_bytes=64)
         w_codes = {}
@@ -229,7 +247,7 @@ def tile_causalselfattention_pa_kernel(tc, x, w_qkv_tern, q_gain, out_0, out_1, 
                 tile = grouped_pool.tile([P, 8 * P], BF16, name="grouped", tag="grouped", align_bytes=64)
                 dst = tile[:].bitcast(F32).rearrange("p (c i u) -> p c u i", i=2, u=2)
                 src = turned[step][b][:].rearrange("p u (c i) -> p c u i", i=2)
-                if step in VECTOR_COPY_STEPS and b == 1:
+                if (step, b) in VECTOR_COPIES:
                     nc.vector.tensor_copy(out=dst, in_=src)
                 else:
                     nc.scalar.copy(out=dst, in_=src)
@@ -277,7 +295,7 @@ def tile_causalselfattention_pa_kernel(tc, x, w_qkv_tern, q_gain, out_0, out_1, 
             for h in range(4):
                 col = 4 * (m % 2) + h
                 nc.scalar.activation(
-                    out=unread_squares[:, col, :],
+                    out=unread_squares[:, (16 * c + 4 * m + h) % 20, :],
                     in_=sums[c, m][:, HEAD * h : HEAD * (h + 1)],
                     func=ACT.Square,
                     accum_out=square_sums[c, pair][:, col : col + 1],
@@ -370,6 +388,8 @@ def tile_causalselfattention_pa_kernel(tc, x, w_qkv_tern, q_gain, out_0, out_1, 
                     closed = (c, m)
             if step < ROW_TILES:
                 transposes(step)
+                if 1 <= step < ROW_TILES - LOADS_AHEAD:
+                    load(step + LOADS_AHEAD)
             if closed is not None:
                 c, m = closed
                 if c < ROPE_CHUNKS:
@@ -397,3 +417,8 @@ def tile_causalselfattention_pa_kernel(tc, x, w_qkv_tern, q_gain, out_0, out_1, 
                 sort_words(step + SORT_AHEAD)
             if step < ROW_TILES:
                 copies(step)
+            if step == SINES_AFTER_STEP:
+                sines()
+                tables()
+            if step == NORM_TABLE_AFTER_STEP:
+                norm_table()

@@ -361,10 +361,11 @@ def tile_causalselfattention_pa_kernel(tc, x, w_qkv_tern, q_gain, out_0, out_1, 
                         op=ALU.add,
                     )
                 else:
-                    nc.vector.tensor_tensor(
+                    adder = nc.gpsimd if c == ROPE_CHUNKS - 1 else nc.vector
+                    adder.tensor_tensor(
                         out=result[:, :, 0:HALF], in0=prod[:, :, 0, 0:HALF], in1=prod[:, :, 1, HALF:HEAD], op=ALU.add
                     )
-                    nc.vector.tensor_tensor(
+                    adder.tensor_tensor(
                         out=result[:, :, HALF:HEAD], in0=prod[:, :, 0, HALF:HEAD], in1=prod[:, :, 1, 0:HALF], op=ALU.add
                     )
                 nc.sync.dma_start(

@@ -29,11 +29,9 @@ Q_HEADS = 16
 LEAD_STEPS = 6
 FIRST_IDLE_MATMULS = 3
 SPLIT_FIRST = True
-VECTOR_SORTS = tuple(range(6, 12))
-SORT_AHEAD = 2
+PAIRS_FROM = 8
 LOADS_AHEAD = 20
 IDLE_STEPS = 5
-LAST_BY_BANK = True
 VECTOR_COPIES = [(0, 1), (1, 1), (5, 0), (5, 1)] + [(s, 1) for s in range(14, 25, 2)]
 SINES_AFTER_STEP = 1
 NORM_TABLE_AFTER_STEP = 4
@@ -83,7 +81,6 @@ def tile_causalselfattention_pa_kernel(tc, x, w_qkv_tern, q_gain, out_0, out_1, 
     with ExitStack() as ctx:
         const = ctx.enter_context(tc.tile_pool(name="const", bufs=1))
         raw_pool = ctx.enter_context(tc.tile_pool(name="raw_pool", bufs=LOADS_AHEAD))
-        sorted_pool = ctx.enter_context(tc.tile_pool(name="sorted_pool", bufs=SORT_AHEAD + 1))
         grouped_pool = ctx.enter_context(tc.tile_pool(name="grouped_pool", bufs=14))
         code_pool = ctx.enter_context(tc.tile_pool(name="code_pool", bufs=3))
         small_pool = ctx.enter_context(tc.tile_pool(name="small_pool", bufs=2 * ROPE_CHUNKS))
@@ -202,7 +199,6 @@ def tile_causalselfattention_pa_kernel(tc, x, w_qkv_tern, q_gain, out_0, out_1, 
         w_codes = {}
         w_scales = {}
 
-        sorted_rows = {}
         turned = {}
         grouped = {}
         sums = {}
@@ -211,32 +207,25 @@ def tile_causalselfattention_pa_kernel(tc, x, w_qkv_tern, q_gain, out_0, out_1, 
         factor = {}
         products = {}
 
-        def sort_words(step):
-            sorted_rows[step] = sorted_pool.tile([P, K], BF16, name="sorted_rows", tag="sorted_rows")
-            nc.vector.tensor_copy(
-                out=sorted_rows[step][:].bitcast(F32).rearrange("p (g u j) -> p g u j", g=PASSES, u=2),
-                in_=raws[step][:].bitcast(F32).rearrange("p (g j u) -> p g u j", g=PASSES, u=2),
-            )
+        def blocks(step, b):
+            if step < PAIRS_FROM:
+                row_tile = order[step]
+                col = P * (row_tile if row_tile < X_TILES else (row_tile - X_TILES) % 4)
+                return [(2 * b, step, col), (2 * b + 1, step, col)]
+            first = step - step % 2
+            g = 2 * (step % 2) + b
+            return [(g, first + j, P * ((order[first] - X_TILES) % 4 + j)) for j in range(2)]
 
         def transposes(step):
             turned[step] = [turn_pool.tile([P, 2, 2 * P], F32, name="turned", tag="turned") for b in range(2)]
-            for g in range(PASSES):
-                if step >= LEAD_STEPS and runs[step - LEAD_STEPS] is None and g % 2 == 0:
-                    nc.tensor.matmul(
-                        out=turned[step][g // 2][:].rearrange("p u c -> p (u c)"),
-                        lhsT=zeros[:, 0:P],
-                        rhs=zeros[:],
-                        start=True,
-                        stop=True,
-                    )
-                for u in range(2):
-                    if step in sorted_rows:
-                        words = sorted_rows[step][:].bitcast(F32)[:, 256 * g + P * u : 256 * g + P * (u + 1)]
-                    elif step == 0 and SPLIT_FIRST:
-                        words = first_raws[g][:].bitcast(F32)[:, u:256:2]
-                    else:
-                        words = raws[step][:].bitcast(F32)[:, 256 * g + u : 256 * (g + 1) : 2]
-                    nc.tensor.transpose(turned[step][g // 2][:, u, P * (g % 2) : P * (g % 2 + 1)], words, ident[:])
+            for b in range(2):
+                for i, (g, source, col) in enumerate(blocks(step, b)):
+                    for u in range(2):
+                        if source == 0 and SPLIT_FIRST:
+                            words = first_raws[g][:].bitcast(F32)[:, u:256:2]
+                        else:
+                            words = raws[source][:].bitcast(F32)[:, 256 * g + u : 256 * (g + 1) : 2]
+                        nc.tensor.transpose(turned[step][b][:, u, P * i : P * (i + 1)], words, ident[:])
             if step < IDLE_STEPS:
                 idle_matmul()
                 idle_matmul()
@@ -256,20 +245,23 @@ def tile_causalselfattention_pa_kernel(tc, x, w_qkv_tern, q_gain, out_0, out_1, 
         def quantise(step):
             row_tile = order[step]
             if row_tile < X_TILES:
-                codes, scales, first_col = x_codes, x_scales, P * row_tile
+                codes, scales = x_codes, x_scales
             else:
                 c = (row_tile - X_TILES) // 4
-                first_col = P * ((row_tile - X_TILES) % 4)
-                if first_col == 0:
+                if c not in w_codes:
                     w_codes[c] = code_pool.tile([P, PASSES, CHUNK], U32, name="w_codes", tag="w_codes", align_bytes=64)
                     w_scales[c] = code_pool.tile([P, PASSES, CHUNK], U8, name="w_scales", tag="w_scales", align_bytes=64)
                 codes, scales = w_codes[c], w_scales[c]
-            for g in range(PASSES):
-                nc.vector.quantize_mx(
-                    out=codes[:, g, first_col : first_col + P].bitcast(E5X4),
-                    scales=scales[:, g, first_col : first_col + P],
-                    in_=grouped[step][g // 2][:, 4 * P * (g % 2) : 4 * P * (g % 2 + 1)],
-                )
+            for b in range(2):
+                parts = blocks(step, b)
+                width = P if step < PAIRS_FROM else 2 * P
+                for i in range(2 * P // width):
+                    g, source, col = parts[i]
+                    nc.vector.quantize_mx(
+                        out=codes[:, g, col : col + width].bitcast(E5X4),
+                        scales=scales[:, g, col : col + width],
+                        in_=grouped[step][b][:, 4 * width * i : 4 * width * (i + 1)],
+                    )
 
         def matmuls(c, m, passes):
             if passes[0] == 0:
@@ -335,22 +327,27 @@ def tile_causalselfattention_pa_kernel(tc, x, w_qkv_tern, q_gain, out_0, out_1, 
                 )
             if m % 2 == 1 and not ADDS_AFTER_QUANT:
                 adds(c, m)
+            if c == ROPE_CHUNKS - 1 and pair == 0:
+                bank_adds(nc.gpsimd, c, m)
+
+        def bank_adds(adder, c, m):
+            prod = products[c, m // 2]
+            rows = slice(4 * (m % 2), 4 * (m % 2) + 4)
+            result = out_pool.tile([P, 4, HEAD], F32, name="result", tag="result")
+            adder.tensor_tensor(
+                out=result[:, :, 0:HALF], in0=prod[:, rows, 0, 0:HALF], in1=prod[:, rows, 1, HALF:HEAD], op=ALU.add
+            )
+            adder.tensor_tensor(
+                out=result[:, :, HALF:HEAD], in0=prod[:, rows, 0, HALF:HEAD], in1=prod[:, rows, 1, 0:HALF], op=ALU.add
+            )
+            nc.sync.dma_start(out=dests[c][P * m : P * (m + 1), :], in_=result[:].rearrange("p h d -> p (h d)"))
 
         def adds(c, m):
             prod = products[c, m // 2]
-            if LAST_BY_BANK and c == ROPE_CHUNKS - 1 and m == TOKEN_TILES - 1:
-                for mm in (m - 1, m):
-                    rows = slice(4 * (mm % 2), 4 * (mm % 2) + 4)
-                    result = out_pool.tile([P, 4, HEAD], F32, name="result", tag="result")
-                    nc.vector.tensor_tensor(
-                        out=result[:, :, 0:HALF], in0=prod[:, rows, 0, 0:HALF], in1=prod[:, rows, 1, HALF:HEAD], op=ALU.add
-                    )
-                    nc.vector.tensor_tensor(
-                        out=result[:, :, HALF:HEAD], in0=prod[:, rows, 0, HALF:HEAD], in1=prod[:, rows, 1, 0:HALF], op=ALU.add
-                    )
-                    nc.sync.dma_start(
-                        out=dests[c][P * mm : P * (mm + 1), :], in_=result[:].rearrange("p h d -> p (h d)")
-                    )
+            if c == ROPE_CHUNKS - 1:
+                if m == TOKEN_TILES - 1:
+                    for mm in (m - 1, m):
+                        bank_adds(nc.vector, c, mm)
             else:
                 result = out_pool.tile([P, 8, HEAD], F32, name="result", tag="result")
                 if MERGED_ADD:
@@ -361,11 +358,10 @@ def tile_causalselfattention_pa_kernel(tc, x, w_qkv_tern, q_gain, out_0, out_1, 
                         op=ALU.add,
                     )
                 else:
-                    adder = nc.gpsimd if c == ROPE_CHUNKS - 1 else nc.vector
-                    adder.tensor_tensor(
+                    nc.vector.tensor_tensor(
                         out=result[:, :, 0:HALF], in0=prod[:, :, 0, 0:HALF], in1=prod[:, :, 1, HALF:HEAD], op=ALU.add
                     )
-                    adder.tensor_tensor(
+                    nc.vector.tensor_tensor(
                         out=result[:, :, HALF:HEAD], in0=prod[:, :, 0, HALF:HEAD], in1=prod[:, :, 1, 0:HALF], op=ALU.add
                     )
                 nc.sync.dma_start(
@@ -414,8 +410,6 @@ def tile_causalselfattention_pa_kernel(tc, x, w_qkv_tern, q_gain, out_0, out_1, 
                     quantise(step - 1)
             if ADDS_AFTER_QUANT and step in rope_due and rope_due[step][1] % 2 == 1:
                 adds(rope_due[step][0], rope_due[step][1])
-            if step + SORT_AHEAD in VECTOR_SORTS:
-                sort_words(step + SORT_AHEAD)
             if step < ROW_TILES:
                 copies(step)
             if step == SINES_AFTER_STEP:

@@ -32,7 +32,7 @@ SPLIT_FIRST = True
 PAIRS_FROM = 8
 LOADS_AHEAD = 20
 IDLE_STEPS = 5
-VECTOR_COPIES = [(0, 1), (1, 1), (5, 0), (5, 1)] + [(s, 1) for s in range(14, 25, 2)]
+VECTOR_COPIES = [(0, 1), (1, 1), (5, 0), (5, 1)] + [(7, 1), (9, 1)] + [(s, 1) for s in range(12, 21, 2)]
 SINES_AFTER_STEP = 1
 NORM_TABLE_AFTER_STEP = 4
 GAIN_LOAD_AFTER = 12
@@ -371,8 +371,11 @@ def tile_causalselfattention_pa_kernel(tc, x, w_qkv_tern, q_gain, out_0, out_1, 
 
         def plain_out(c, m):
             plain = plain_pool.tile([P, CHUNK], F32, name="plain", tag="plain")
-            nc.scalar.copy(out=plain[:], in_=sums[c, m][:])
-            nc.scalar.dma_start(out=dests[c][P * m : P * (m + 1), :], in_=plain[:])
+            pieces = 2 if m == TOKEN_TILES - 1 else 1
+            for i in range(pieces):
+                cols = slice(CHUNK // pieces * i, CHUNK // pieces * (i + 1))
+                nc.scalar.copy(out=plain[:, cols], in_=sums[c, m][:, cols])
+                nc.scalar.dma_start(out=dests[c][P * m : P * (m + 1), cols], in_=plain[:, cols])
 
         factors_due = {}
         rope_due = {}

@@ -32,16 +32,16 @@ SPLIT_FIRST = True
 PAIRS_FROM = 8
 LOADS_AHEAD = 20
 IDLE_STEPS = 5
-VECTOR_COPIES = [(0, 1), (1, 1), (5, 0), (5, 1)] + [(7, 1), (9, 1)] + [(s, 1) for s in range(12, 21, 2)]
+VECTOR_COPIES = [(0, 1), (1, 1), (5, 0), (5, 1)] + [(s, 1) for s in range(7, 14, 2)] + [(s, 1) for s in range(16, 21, 2)]
 SINES_AFTER_STEP = 1
 NORM_TABLE_AFTER_STEP = 4
-GAIN_LOAD_AFTER = 12
-ADDS_AFTER_QUANT = True
+GAIN_LOAD_AFTER = 8
 MERGED_ADD = False
 EARLY = 0
 Q_BEFORE_FIRST_PRODUCTS = True
 TURN_BUFS = 4
 SUM_BUFS = 4
+GPSIMD_PAIRS = ((3, 1), (4, 0))
 
 RMS_EPS = 1.1920929e-07
 PI = 3.141592653589793
@@ -280,6 +280,11 @@ def tile_causalselfattention_pa_kernel(tc, x, w_qkv_tern, q_gain, out_0, out_1, 
                     stop=(g == PASSES - 1),
                 )
 
+        def banks_with(c, m):
+            if c == 0:
+                return [m % 2]
+            return [0, 1] if m % 2 == 1 else []
+
         def squares(c, m):
             pair = m // 2
             if m % 2 == 0:
@@ -292,22 +297,28 @@ def tile_causalselfattention_pa_kernel(tc, x, w_qkv_tern, q_gain, out_0, out_1, 
                     func=ACT.Square,
                     accum_out=square_sums[c, pair][:, col : col + 1],
                 )
-            if m % 2 == 1:
-                rstd[c, pair] = small_pool.tile([P, 8], F32, name="rstd", tag="rstd")
+            banks = banks_with(c, m)
+            if len(banks) > 0:
+                if banks[0] == 0:
+                    rstd[c, pair] = small_pool.tile([P, 8], F32, name="rstd", tag="rstd")
+                cols = slice(4 * banks[0], 4 * banks[-1] + 4)
                 nc.scalar.activation(
-                    out=rstd[c, pair][:],
-                    in_=square_sums[c, pair][:],
+                    out=rstd[c, pair][:, cols],
+                    in_=square_sums[c, pair][:, cols],
                     func=ACT.Abs_reciprocal_sqrt,
                     scale=1.0 / HEAD,
                     bias=RMS_EPS,
                 )
 
-        def factors(c, pair):
-            factor[c, pair] = small_pool.tile([P, 2, 4], F32, name="factor", tag="factor")
+        def factors(c, m):
+            pair = m // 2
+            banks = banks_with(c, m)
+            if banks[0] == 0:
+                factor[c, pair] = small_pool.tile([P, 2, 4], F32, name="factor", tag="factor")
             nc.vector.tensor_tensor(
-                out=factor[c, pair][:],
-                in0=rstd[c, pair][:].rearrange("p (m h) -> p m h", m=2),
-                in1=gain[:, 4 * c : 4 * c + 4].unsqueeze(1).to_broadcast([P, 2, 4]),
+                out=factor[c, pair][:, banks[0] : banks[-1] + 1, :],
+                in0=rstd[c, pair][:].rearrange("p (m h) -> p m h", m=2)[:, banks[0] : banks[-1] + 1, :],
+                in1=gain[:, 4 * c : 4 * c + 4].unsqueeze(1).to_broadcast([P, len(banks), 4]),
                 op=ALU.mult,
             )
 
@@ -325,9 +336,7 @@ def tile_causalselfattention_pa_kernel(tc, x, w_qkv_tern, q_gain, out_0, out_1, 
                     op0=ALU.mult,
                     op1=ALU.mult,
                 )
-            if m % 2 == 1 and not ADDS_AFTER_QUANT:
-                adds(c, m)
-            if c == ROPE_CHUNKS - 1 and pair == 0:
+            if (c, pair) in GPSIMD_PAIRS:
                 bank_adds(nc.gpsimd, c, m)
 
         def bank_adds(adder, c, m):
@@ -344,11 +353,10 @@ def tile_causalselfattention_pa_kernel(tc, x, w_qkv_tern, q_gain, out_0, out_1, 
 
         def adds(c, m):
             prod = products[c, m // 2]
-            if c == ROPE_CHUNKS - 1:
-                if m == TOKEN_TILES - 1:
-                    for mm in (m - 1, m):
-                        bank_adds(nc.vector, c, mm)
-            else:
+            if c == ROPE_CHUNKS - 1 and m == TOKEN_TILES - 1:
+                for mm in (m - 1, m):
+                    bank_adds(nc.vector, c, mm)
+            elif (c, m // 2) not in GPSIMD_PAIRS:
                 result = out_pool.tile([P, 8, HEAD], F32, name="result", tag="result")
                 if MERGED_ADD:
                     nc.vector.tensor_tensor(
@@ -379,6 +387,7 @@ def tile_causalselfattention_pa_kernel(tc, x, w_qkv_tern, q_gain, out_0, out_1, 
 
         factors_due = {}
         rope_due = {}
+        adds_due = {}
         for step in range(LEAD_STEPS + len(runs) + 3):
             closed = None
             if 0 <= step - LEAD_STEPS < len(runs) and runs[step - LEAD_STEPS] is not None:
@@ -394,10 +403,16 @@ def tile_causalselfattention_pa_kernel(tc, x, w_qkv_tern, q_gain, out_0, out_1, 
                 c, m = closed
                 if c < ROPE_CHUNKS:
                     squares(c, m)
-                    if m % 2 == 1:
-                        factors_due[step + 1] = (c, m // 2)
+                    if c == 0:
+                        factors_due[step + 1] = (c, m)
+                        rope_due[step + 1] = (c, m)
+                        if m % 2 == 1:
+                            adds_due[step + 2] = (c, m)
+                    elif m % 2 == 1:
+                        factors_due[step + 1] = (c, m)
                         rope_due[step + 1] = (c, m - 1)
                         rope_due[step + 2] = (c, m)
+                        adds_due[step + 2] = (c, m)
                 else:
                     plain_out(c, m)
             if step in factors_due:
@@ -411,8 +426,8 @@ def tile_causalselfattention_pa_kernel(tc, x, w_qkv_tern, q_gain, out_0, out_1, 
                     rope(rope_due[step][0], rope_due[step][1])
                 if 1 <= step <= ROW_TILES:
                     quantise(step - 1)
-            if ADDS_AFTER_QUANT and step in rope_due and rope_due[step][1] % 2 == 1:
-                adds(rope_due[step][0], rope_due[step][1])
+            if step in adds_due:
+                adds(adds_due[step][0], adds_due[step][1])
             if step < ROW_TILES:
                 copies(step)
             if step == SINES_AFTER_STEP:

from contextlib import ExitStack

import concourse.mybir as mybir
from concourse.masks import make_identity

F32 = mybir.dt.float32
BF16 = mybir.dt.bfloat16
I32 = mybir.dt.int32
U32 = mybir.dt.uint32
U8 = mybir.dt.uint8
E5X4 = mybir.dt.float8_e5m2_x4
ACT = mybir.ActivationFunctionType
ALU = mybir.AluOpType

P = 128
K = 2048
PASSES = 4
TOKENS = 512
TOKEN_TILES = 4
HEAD = 128
HALF = 64
CHUNK = 512
CHUNKS = 6
ROPE_CHUNKS = 5
X_TILES = 4
ROW_TILES = 28
Q_HEADS = 16

LEAD_STEPS = 6
FIRST_IDLE_MATMULS = 3
SPLIT_FIRST = True
PAIRS_FROM = 8
LOADS_AHEAD = 20
IDLE_STEPS = 5
VECTOR_COPIES = [(0, 1), (1, 1), (5, 0), (5, 1)] + [(s, 1) for s in range(7, 14, 2)] + [(s, 1) for s in range(16, 21, 2)]
SINES_AFTER_STEP = 1
NORM_TABLE_AFTER_STEP = 4
GAIN_LOAD_AFTER = 8
MERGED_ADD = False
EARLY = 0
Q_BEFORE_FIRST_PRODUCTS = True
TURN_BUFS = 4
SUM_BUFS = 4
GPSIMD_PAIRS = ((3, 1), (4, 0))

RMS_EPS = 1.1920929e-07
PI = 3.141592653589793
PI_HI = 102944.0 / 32768.0
PI_LO = PI - PI_HI
FREQ_RATIO = 10000.0 ** (-1.0 / 64.0)

FLOPS = 2 * TOKENS * K * CHUNK * CHUNKS


def tile_causalselfattention_pa_kernel(tc, x, w_qkv_tern, q_gain, out_0, out_1, out_2):
    nc = tc.nc

    x_rows = x.rearrange("b s k -> (b s) k")
    row_tiles = [x_rows[P * i : P * (i + 1), :] for i in range(X_TILES)]
    row_tiles.extend([w_qkv_tern[P * i : P * (i + 1), :] for i in range(ROW_TILES - X_TILES)])
    q_flat = out_0.rearrange("b s h d -> (b s) (h d)")
    dests = [q_flat[:, CHUNK * c : CHUNK * (c + 1)] for c in range(4)]
    dests.append(out_1.rearrange("b s h d -> (b s) (h d)"))
    dests.append(out_2.rearrange("b s h d -> (b s) (h d)"))

    order = [0, 4, 5, 6, 7, 1, 2, 3]
    order.extend(range(8, ROW_TILES))
    runs = []
    for m in range(TOKEN_TILES):
        if m < EARLY:
            runs.append((0, m, (0, 1, 2, 3)))
        else:
            runs.append((0, m, (0, 1)))
            runs.append((0, m, (2, 3)))
    for m in range(EARLY):
        runs.append(None)
    for c in range(1, CHUNKS):
        for m in range(TOKEN_TILES):
            runs.append((c, m, (0, 1, 2, 3)))

    with ExitStack() as ctx:
        const = ctx.enter_context(tc.tile_pool(name="const", bufs=1))
        raw_pool = ctx.enter_context(tc.tile_pool(name="raw_pool", bufs=LOADS_AHEAD))
        grouped_pool = ctx.enter_context(tc.tile_pool(name="grouped_pool", bufs=14))
        code_pool = ctx.enter_context(tc.tile_pool(name="code_pool", bufs=3))
        small_pool = ctx.enter_context(tc.tile_pool(name="small_pool", bufs=2 * ROPE_CHUNKS))
        out_pool = ctx.enter_context(tc.tile_pool(name="out_pool", bufs=5))
        plain_pool = ctx.enter_context(tc.tile_pool(name="plain_pool", bufs=TOKEN_TILES))
        turn_pool = ctx.enter_context(tc.psum_pool(name="turn_pool", bufs=TURN_BUFS))
        sum_pool = ctx.enter_context(tc.psum_pool(name="sum_pool", bufs=SUM_BUFS))
        ctx.enter_context(tc.manual_schedule())

        gain_bf = const.tile([P, Q_HEADS], BF16, name="gain_bf")
        raws = []
        first_raws = []

        def load(step):
            raw = raw_pool.tile([P, K], BF16, name="raw", tag="raw")
            nc.sync.dma_start(out=raw[:], in_=row_tiles[order[step]])
            raws.append(raw)

        for step in range(LOADS_AHEAD + 1):
            if step == 0 and SPLIT_FIRST:
                for g in range(PASSES):
                    piece = const.tile([P, K // PASSES], BF16, name="first_raw%d" % g)
                    nc.sync.dma_start(
                        out=piece[:], in_=row_tiles[order[0]][:, (K // PASSES) * g : (K // PASSES) * (g + 1)]
                    )
                    first_raws.append(piece)
                raws.append(None)
                continue
            load(step)
            if step == GAIN_LOAD_AFTER - 1:
                nc.sync.dma_start(out=gain_bf[:], in_=q_gain.partition_broadcast(P))

        zeros = const.tile([P, CHUNK], BF16, name="zeros")
        nc.vector.memset(zeros[:], 0.0)
        idle_sum = sum_pool.tile([P, CHUNK], F32, name="sums", tag="sums")

        def idle_matmul():
            nc.tensor.matmul(out=idle_sum[:], lhsT=zeros[:, 0:P], rhs=zeros[:], start=True, stop=True)

        for i in range(FIRST_IDLE_MATMULS):
            idle_matmul()

        token = const.tile([P, TOKEN_TILES], I32, name="token")
        nc.gpsimd.iota(token[:], pattern=[[P, TOKEN_TILES]], base=0, channel_multiplier=1)
        ident = const.tile([P, P], F32, name="ident")
        make_identity(nc, ident[:])
        gain = const.tile([P, Q_HEADS + 4], F32, name="gain")
        nc.gpsimd.memset(gain[:], 1.0)

        half_angle = const.tile([P, TOKEN_TILES, HALF], F32, name="half_angle")
        nc.vector.tensor_scalar(
            out=half_angle[:, :, 0:1], in0=token[:].unsqueeze(2), scalar1=0.5, scalar2=None, op0=ALU.mult
        )
        for width in (1, 4, 16):
            for i in range(1, 4):
                nc.vector.tensor_scalar(
                    out=half_angle[:, :, i * width : (i + 1) * width],
                    in0=half_angle[:, :, 0:width],
                    scalar1=FREQ_RATIO ** (i * width),
                    scalar2=None,
                    op0=ALU.mult,
                )
        turns = const.tile([P, TOKEN_TILES, HALF], I32, name="turns")
        nc.vector.tensor_scalar(
            out=turns[:], in0=half_angle[:], scalar1=1.0 / PI, scalar2=0.1, op0=ALU.mult, op1=ALU.add
        )
        reduced_hi = const.tile([P, TOKEN_TILES, HALF], F32, name="reduced_hi")
        nc.vector.scalar_tensor_tensor(
            out=reduced_hi[:], in0=turns[:], scalar=-PI_HI, in1=half_angle[:], op0=ALU.mult, op1=ALU.add
        )
        reduced = const.tile([P, TOKEN_TILES, HALF], F32, name="reduced")
        nc.vector.scalar_tensor_tensor(
            out=reduced[:], in0=turns[:], scalar=-PI_LO, in1=reduced_hi[:], op0=ALU.mult, op1=ALU.add
        )
        sin_for_cos = const.tile([P, TOKEN_TILES, HALF], F32, name="sin_for_cos")
        sin_for_sin = const.tile([P, TOKEN_TILES, HALF], F32, name="sin_for_sin")
        first_call = const.tile([P, 2], F32, name="first_call")
        nc.scalar.activation(out=first_call[:, 0:1], in_=gain[:, Q_HEADS : Q_HEADS + 1], func=ACT.Sin)

        def sines():
            nc.scalar.activation(out=sin_for_cos[:], in_=reduced[:], func=ACT.Sin)
            nc.scalar.activation(out=sin_for_sin[:], in_=reduced[:], func=ACT.Sin, bias=-PI / 4.0)

        def norm_table():
            nc.scalar.activation(
                out=first_call[:, 1:2], in_=gain[:, Q_HEADS : Q_HEADS + 1], func=ACT.Abs_reciprocal_sqrt
            )

        square_for_cos = const.tile([P, TOKEN_TILES, HALF], F32, name="square_for_cos")
        square_for_sin = const.tile([P, TOKEN_TILES, HALF], F32, name="square_for_sin")
        table = const.tile([P, TOKEN_TILES, 2, HEAD], F32, name="table")

        def tables():
            nc.gpsimd.tensor_tensor(out=square_for_cos[:], in0=sin_for_cos[:], in1=sin_for_cos[:], op=ALU.mult)
            nc.gpsimd.tensor_tensor(out=square_for_sin[:], in0=sin_for_sin[:], in1=sin_for_sin[:], op=ALU.mult)
            for row, first_col, square, sign in (
                (0, 0, square_for_cos, 1.0),
                (0, HALF, square_for_cos, 1.0),
                (1, 0, square_for_sin, -1.0),
                (1, HALF, square_for_sin, 1.0),
            ):
                nc.gpsimd.tensor_scalar(
                    out=table[:, :, row, first_col : first_col + HALF],
                    in0=square[:],
                    scalar1=-2.0 * sign,
                    scalar2=sign,
                    op0=ALU.mult,
                    op1=ALU.add,
                )
            nc.gpsimd.tensor_copy(out=gain[:, 0:Q_HEADS], in_=gain_bf[:])


        unread_squares = const.tile([P, 20, HEAD], BF16, name="unread_squares")
        x_codes = const.tile([P, PASSES, TOKENS], U32, name="x_codes", align_bytes=64)
        x_scales = const.tile([P, PASSES, TOKENS], U8, name="x_scales", align_bytes=64)
        w_codes = {}
        w_scales = {}

        turned = {}
        grouped = {}
        sums = {}
        square_sums = {}
        rstd = {}
        factor = {}
        products = {}

        def blocks(step, b):
            if step < PAIRS_FROM:
                row_tile = order[step]
                col = P * (row_tile if row_tile < X_TILES else (row_tile - X_TILES) % 4)
                return [(2 * b, step, col), (2 * b + 1, step, col)]
            first = step - step % 2
            g = 2 * (step % 2) + b
            return [(g, first + j, P * ((order[first] - X_TILES) % 4 + j)) for j in range(2)]

        def transposes(step):
            turned[step] = [turn_pool.tile([P, 2, 2 * P], F32, name="turned", tag="turned") for b in range(2)]
            for b in range(2):
                for i, (g, source, col) in enumerate(blocks(step, b)):
                    for u in range(2):
                        if source == 0 and SPLIT_FIRST:
                            words = first_raws[g][:].bitcast(F32)[:, u:256:2]
                        else:
                            words = raws[source][:].bitcast(F32)[:, 256 * g + u : 256 * (g + 1) : 2]
                        nc.tensor.transpose(turned[step][b][:, u, P * i : P * (i + 1)], words, ident[:])
            if step < IDLE_STEPS:
                idle_matmul()
                idle_matmul()

        def copies(step):
            grouped[step] = []
            for b in range(2):
                tile = grouped_pool.tile([P, 8 * P], BF16, name="grouped", tag="grouped", align_bytes=64)
                dst = tile[:].bitcast(F32).rearrange("p (c i u) -> p c u i", i=2, u=2)
                src = turned[step][b][:].rearrange("p u (c i) -> p c u i", i=2)
                if (step, b) in VECTOR_COPIES:
                    nc.vector.tensor_copy(out=dst, in_=src)
                else:
                    nc.scalar.copy(out=dst, in_=src)
                grouped[step].append(tile)

        def quantise(step):
            row_tile = order[step]
            if row_tile < X_TILES:
                codes, scales = x_codes, x_scales
            else:
                c = (row_tile - X_TILES) // 4
                if c not in w_codes:
                    w_codes[c] = code_pool.tile([P, PASSES, CHUNK], U32, name="w_codes", tag="w_codes", align_bytes=64)
                    w_scales[c] = code_pool.tile([P, PASSES, CHUNK], U8, name="w_scales", tag="w_scales", align_bytes=64)
                codes, scales = w_codes[c], w_scales[c]
            for b in range(2):
                parts = blocks(step, b)
                width = P if step < PAIRS_FROM else 2 * P
                for i in range(2 * P // width):
                    g, source, col = parts[i]
                    nc.vector.quantize_mx(
                        out=codes[:, g, col : col + width].bitcast(E5X4),
                        scales=scales[:, g, col : col + width],
                        in_=grouped[step][b][:, 4 * width * i : 4 * width * (i + 1)],
                    )

        def matmuls(c, m, passes):
            if passes[0] == 0:
                if c < ROPE_CHUNKS:
                    sums[c, m] = sum_pool.tile([P, CHUNK], F32, name="sums", tag="sums")
                else:
                    sums[c, m] = turn_pool.tile([P, CHUNK], F32, name="turned", tag="turned")
            for g in passes:
                nc.tensor.matmul_mx(
                    out=sums[c, m][:],
                    lhsT=x_codes[:, g, P * m : P * (m + 1)].bitcast(E5X4),
                    lhsT_scale=x_scales[:, g, P * m : P * (m + 1)],
                    rhs=w_codes[c][:, g, :].bitcast(E5X4),
                    rhs_scale=w_scales[c][:, g, :],
                    start=(g == 0),
                    stop=(g == PASSES - 1),
                )

        def banks_with(c, m):
            if c == 0:
                return [m % 2]
            return [0, 1] if m % 2 == 1 else []

        def squares(c, m):
            pair = m // 2
            if m % 2 == 0:
                square_sums[c, pair] = small_pool.tile([P, 8], F32, name="square_sums", tag="square_sums")
            for h in range(4):
                col = 4 * (m % 2) + h
                nc.scalar.activation(
                    out=unread_squares[:, (16 * c + 4 * m + h) % 20, :],
                    in_=sums[c, m][:, HEAD * h : HEAD * (h + 1)],
                    func=ACT.Square,
                    accum_out=square_sums[c, pair][:, col : col + 1],
                )
            banks = banks_with(c, m)
            if len(banks) > 0:
                if banks[0] == 0:
                    rstd[c, pair] = small_pool.tile([P, 8], F32, name="rstd", tag="rstd")
                cols = slice(4 * banks[0], 4 * banks[-1] + 4)
                nc.scalar.activation(
                    out=rstd[c, pair][:, cols],
                    in_=square_sums[c, pair][:, cols],
                    func=ACT.Abs_reciprocal_sqrt,
                    scale=1.0 / HEAD,
                    bias=RMS_EPS,
                )

        def factors(c, m):
            pair = m // 2
            banks = banks_with(c, m)
            if banks[0] == 0:
                factor[c, pair] = small_pool.tile([P, 2, 4], F32, name="factor", tag="factor")
            nc.vector.tensor_tensor(
                out=factor[c, pair][:, banks[0] : banks[-1] + 1, :],
                in0=rstd[c, pair][:].rearrange("p (m h) -> p m h", m=2)[:, banks[0] : banks[-1] + 1, :],
                in1=gain[:, 4 * c : 4 * c + 4].unsqueeze(1).to_broadcast([P, len(banks), 4]),
                op=ALU.mult,
            )

        def rope(c, m):
            pair = m // 2
            if m % 2 == 0:
                products[c, pair] = small_pool.tile([P, 8, 2, HEAD], F32, name="products", tag="products", bufs=2)
            prod = products[c, pair]
            for h in range(4):
                nc.vector.scalar_tensor_tensor(
                    out=prod[:, 4 * (m % 2) + h, :, :],
                    in0=sums[c, m][:, HEAD * h : HEAD * (h + 1)].unsqueeze(1).to_broadcast([P, 2, HEAD]),
                    scalar=factor[c, pair][:, m % 2, h : h + 1],
                    in1=table[:, m, :, :],
                    op0=ALU.mult,
                    op1=ALU.mult,
                )
            if (c, pair) in GPSIMD_PAIRS:
                bank_adds(nc.gpsimd, c, m)

        def bank_adds(adder, c, m):
            prod = products[c, m // 2]
            rows = slice(4 * (m % 2), 4 * (m % 2) + 4)
            result = out_pool.tile([P, 4, HEAD], F32, name="result", tag="result")
            adder.tensor_tensor(
                out=result[:, :, 0:HALF], in0=prod[:, rows, 0, 0:HALF], in1=prod[:, rows, 1, HALF:HEAD], op=ALU.add
            )
            adder.tensor_tensor(
                out=result[:, :, HALF:HEAD], in0=prod[:, rows, 0, HALF:HEAD], in1=prod[:, rows, 1, 0:HALF], op=ALU.add
            )
            nc.sync.dma_start(out=dests[c][P * m : P * (m + 1), :], in_=result[:].rearrange("p h d -> p (h d)"))

        def adds(c, m):
            prod = products[c, m // 2]
            if c == ROPE_CHUNKS - 1 and m == TOKEN_TILES - 1:
                for mm in (m - 1, m):
                    bank_adds(nc.vector, c, mm)
            elif (c, m // 2) not in GPSIMD_PAIRS:
                result = out_pool.tile([P, 8, HEAD], F32, name="result", tag="result")
                if MERGED_ADD:
                    nc.vector.tensor_tensor(
                        out=result[:].rearrange("p h (f j) -> p h f j", f=2),
                        in0=prod[:, :, 0, :].rearrange("p h (f j) -> p h f j", f=2),
                        in1=prod[:, :, 1, :].rearrange("p h (f j) -> p h f j", f=2)[:, :, ::-1, :],
                        op=ALU.add,
                    )
                else:
                    nc.vector.tensor_tensor(
                        out=result[:, :, 0:HALF], in0=prod[:, :, 0, 0:HALF], in1=prod[:, :, 1, HALF:HEAD], op=ALU.add
                    )
                    nc.vector.tensor_tensor(
                        out=result[:, :, HALF:HEAD], in0=prod[:, :, 0, HALF:HEAD], in1=prod[:, :, 1, 0:HALF], op=ALU.add
                    )
                nc.sync.dma_start(
                    out=dests[c].rearrange("(m p) n -> p m n", p=P)[:, m - 1 : m + 1, :],
                    in_=result[:].rearrange("p (m h) d -> p m (h d)", m=2),
                )

        def plain_out(c, m):
            plain = plain_pool.tile([P, CHUNK], F32, name="plain", tag="plain")
            pieces = 2 if m == TOKEN_TILES - 1 else 1
            for i in range(pieces):
                cols = slice(CHUNK // pieces * i, CHUNK // pieces * (i + 1))
                nc.scalar.copy(out=plain[:, cols], in_=sums[c, m][:, cols])
                nc.scalar.dma_start(out=dests[c][P * m : P * (m + 1), cols], in_=plain[:, cols])

        factors_due = {}
        rope_due = {}
        adds_due = {}
        for step in range(LEAD_STEPS + len(runs) + 3):
            closed = None
            if 0 <= step - LEAD_STEPS < len(runs) and runs[step - LEAD_STEPS] is not None:
                c, m, passes = runs[step - LEAD_STEPS]
                matmuls(c, m, passes)
                if passes[-1] == PASSES - 1:
                    closed = (c, m)
            if step < ROW_TILES:
                transposes(step)
                if 1 <= step < ROW_TILES - LOADS_AHEAD:
                    load(step + LOADS_AHEAD)
            if closed is not None:
                c, m = closed
                if c < ROPE_CHUNKS:
                    squares(c, m)
                    if c == 0:
                        factors_due[step + 1] = (c, m)
                        rope_due[step + 1] = (c, m)
                        if m % 2 == 1:
                            adds_due[step + 2] = (c, m)
                    elif m % 2 == 1:
                        factors_due[step + 1] = (c, m)
                        rope_due[step + 1] = (c, m - 1)
                        rope_due[step + 2] = (c, m)
                        adds_due[step + 2] = (c, m)
                else:
                    plain_out(c, m)
            if step in factors_due:
                factors(factors_due[step][0], factors_due[step][1])
            if Q_BEFORE_FIRST_PRODUCTS and step in factors_due:
                if 1 <= step <= ROW_TILES:
                    quantise(step - 1)
                rope(rope_due[step][0], rope_due[step][1])
            else:
                if step in rope_due:
                    rope(rope_due[step][0], rope_due[step][1])
                if 1 <= step <= ROW_TILES:
                    quantise(step - 1)
            if step in adds_due:
                adds(adds_due[step][0], adds_due[step][1])
            if step < ROW_TILES:
                copies(step)
            if step == SINES_AFTER_STEP:
                sines()
                tables()
            if step == NORM_TABLE_AFTER_STEP:
                norm_table()
